import numpy as np
import ml_dtypes


def mxq(x, axis, fmt="e4m3"):
    dtype, down = {"e4m3": (ml_dtypes.float8_e4m3fn, 7), "e5m2": (ml_dtypes.float8_e5m2, 14)}[fmt]
    v = np.moveaxis(np.asarray(x, np.float32).astype(ml_dtypes.bfloat16).astype(np.float64), axis, -1)
    blocks = v.reshape(v.shape[:-1] + (-1, 32))
    amax = np.abs(blocks).max(-1, keepdims=True)
    byte = np.maximum(np.where(amax > 0, np.frexp(amax)[1] - 1 + 127, 0) - down, 1)
    scale = np.exp2(byte - 127.0)
    codes = (blocks / scale).astype(np.float32).astype(dtype).astype(np.float64)
    return np.moveaxis((codes * scale).reshape(v.shape), -1, axis)


WIDE = False


def mx_kscale(k):
    if not WIDE:
        return np.ones(k)
    levels = np.array([10, -10, 5, -5, 0])
    a = np.random.permutation(np.resize(levels, k // 512 * 4)).reshape(k // 512, 4)
    idx = np.arange(k)
    return np.exp2(a[idx // 512, idx % 128 // 32])


BF16 = ml_dtypes.bfloat16


def bf(x):
    return np.asarray(x, np.float32).astype(BF16)


def f64(x):
    return np.asarray(x).astype(np.float64)


B, N, D = 4, 512, 512
C = 2 * D
EPS_L1 = 1e-12
EPS_BN = 1e-5
NEG_SLOPE = 0.01


def l1_normalize(x):
    return x / np.maximum(np.sum(np.abs(x), axis=-1, keepdims=True), EPS_L1)


def bn_lrelu(x, g, b):
    mean = np.mean(x, axis=(0, 2), keepdims=True)
    var = np.var(x, axis=(0, 2), keepdims=True)
    y = (x - mean) / np.sqrt(var + EPS_BN) * g[None, :, None] + b[None, :, None]
    return np.where(y >= 0, y, NEG_SLOPE * y)


def draw_edge():
    u = 1.5 * np.random.random_sample((B, N, N)) - 0.5 + 2.0 * np.eye(N)
    return bf(u * np.exp(0.5 * np.random.standard_normal((B, N, 1))))


def setup_inputs():
    t = mx_kscale(C)[:D]
    tt = np.concatenate([t, t])
    return {"distribution_edge": draw_edge(),
            "instance_edge": draw_edge(),
            "point_node": bf(np.random.standard_normal((B, N, D)) * 0.2 * np.sqrt(N) * t),
            "W1": bf(np.random.standard_normal((C, C)) * 2.0 / np.sqrt(C) / tt[None, :]),
            "g1": bf(1.0 + 0.2 * np.random.standard_normal(C)),
            "b1": bf(0.3 * np.random.standard_normal(C))}


def reference(distribution_edge, instance_edge, point_node, W1, g1, b1):
    diag_mask = 1.0 - np.eye(N)
    pq = mxq(f64(point_node), 1, "e4m3")
    edge_feat = l1_normalize(f64(distribution_edge) * diag_mask)
    aggr_feat = mxq(edge_feat, 2, "e4m3") @ pq
    edge_instance = l1_normalize(f64(instance_edge) * diag_mask)
    aggr_instance = mxq(edge_instance, 2, "e4m3") @ pq
    x = np.concatenate([aggr_feat, aggr_instance], axis=-1)
    x = np.swapaxes(x, 1, 2)
    z = mxq(f64(W1), 1, "e4m3") @ mxq(x, 1, "e4m3")
    return bn_lrelu(z, f64(g1), f64(b1))

@@ -1,0 +1,264 @@
+from contextlib import ExitStack
+
+import concourse.mybir as mybir
+from concourse.masks import make_identity
+
+F32 = mybir.dt.float32
+BF16 = mybir.dt.bfloat16
+U32 = mybir.dt.uint32
+U8 = mybir.dt.uint8
+FP8X4 = mybir.dt.float8_e4m3fn_x4
+ALU = mybir.AluOpType
+ACT = mybir.ActivationFunctionType
+
+P = 128
+B = 4
+N = 512
+D = 512
+C = 1024
+NO = C // P
+NU = 2 * B
+EPS_L1 = 1e-12
+EPS_BN = 1e-5
+NEG_SLOPE = 0.01
+
+FLOPS = 2 * (2 * B * N * N * D) + 2 * B * C * C * N
+
+
+def tile_yuyipointupdate_pa_kernel(tc, distribution_edge, instance_edge, point_node, W1, g1, b1, out):
+    nc = tc.nc
+    edges = (distribution_edge, instance_edge)
+    with ExitStack() as ctx:
+        const = ctx.enter_context(tc.tile_pool(name="const", bufs=1))
+        raw = ctx.enter_context(tc.tile_pool(name="raw", bufs=1))
+        keep = ctx.enter_context(tc.tile_pool(name="keep", bufs=1))
+        work = ctx.enter_context(tc.tile_pool(name="work", bufs=3))
+        small = ctx.enter_context(tc.tile_pool(name="small", bufs=4))
+        ypool = ctx.enter_context(tc.tile_pool(name="ypool", bufs=2))
+        tp = ctx.enter_context(tc.psum_pool(name="tp", bufs=3))
+        mm = ctx.enter_context(tc.psum_pool(name="mm", bufs=5))
+
+        er = {}
+        pr = {}
+
+        def load_edge(u):
+            t = raw.tile([P, 4, N], BF16, name="er%d" % u)
+            nc.sync.dma_start(out=t[:], in_=edges[u % 2][u // 2].rearrange("(T p) m -> p T m", p=P))
+            er[u] = t
+
+        def load_pn(b):
+            t = raw.tile([P, 4, D], BF16, name="pr%d" % b)
+            nc.sync.dma_start(out=t[:], in_=point_node[b].rearrange("(t p) f -> p t f", p=P))
+            pr[b] = t
+
+        gb = const.tile([P, P], BF16, name="gb")
+        nc.vector.memset(gb[:], 0.0)
+        nc.scalar.dma_start(out=gb[0:NO, :], in_=g1.rearrange("(o p) -> o p", p=P))
+        nc.scalar.dma_start(out=gb[NO:2 * NO, :], in_=b1.rearrange("(o p) -> o p", p=P))
+
+        load_edge(0)
+        load_pn(0)
+        load_edge(1)
+        wr = raw.tile([P, NO, C], BF16, name="wr")
+        w_view = W1.rearrange("(O p) c -> p O c", p=P)
+        nc.sync.dma_start(out=wr[:, 0:4, :], in_=w_view[:, 0:4, :])
+        nc.sync.dma_start(out=wr[:, 4:8, :], in_=w_view[:, 4:8, :])
+        for b in range(1, B):
+            load_edge(2 * b)
+            load_pn(b)
+            load_edge(2 * b + 1)
+
+        ident_bf = const.tile([P, P], BF16, name="ident_bf")
+        make_identity(nc, ident_bf[:])
+        ident_f = const.tile([P, P], F32, name="ident_f")
+        make_identity(nc, ident_f[:])
+        offd = const.tile([P, P], BF16, name="offd")
+        nc.vector.tensor_scalar(out=offd[:], in0=ident_bf[:], scalar1=-1.0, scalar2=1.0, op0=ALU.mult, op1=ALU.add)
+        eps_t = const.tile([P, 1], F32, name="eps_t")
+        nc.vector.memset(eps_t[:], EPS_BN)
+        junk = const.tile([P, N], BF16, name="junk")
+        junk1 = const.tile([P, 1], F32, name="junk1")
+        st = const.tile([P, NO, B, 6], F32, name="st")
+
+        gps = tp.tile([P, P], BF16, name="gps", tag="tp")
+        nc.tensor.transpose(gps[:], gb[:], ident_bf[:])
+        gbT = const.tile([P, 2 * NO], F32, name="gbT")
+        nc.vector.tensor_copy(out=gbT[:], in_=gps[:, 0:2 * NO])
+
+        pc = {}
+        ps = {}
+        xc = {}
+        xs = {}
+        ecs = {}
+        rss = {}
+
+        def copy_on(engine, dst, src):
+            if engine == "S":
+                nc.scalar.copy(out=dst, in_=src)
+            else:
+                nc.vector.tensor_copy(out=dst, in_=src)
+
+        def pn_prep(b):
+            png = work.tile([P, D, 4], BF16, name="png", align_bytes=64, bufs=2)
+            dst = png[:].rearrange("q (u e p) t -> q u e p t", u=2, e=2)
+            src = pr[b][:].rearrange("q t (u p e) -> q u e p t", u=2, e=2)
+            for u in range(2):
+                nc.vector.tensor_copy(out=dst[:, u], in_=src[:, u])
+            pc[b] = keep.tile([P, D], U32, name="pc%d" % b, align_bytes=64)
+            ps[b] = keep.tile([P, D], U8, name="ps%d" % b, align_bytes=64)
+            nc.vector.quantize_mx(out=pc[b][:].bitcast(FP8X4), scales=ps[b][:], in_=png[:].rearrange("q c t -> q (c t)"))
+            xc[b] = keep.tile([P, 2, N], U32, name="xc%d" % b, align_bytes=64)
+            xs[b] = keep.tile([P, 2, N], U8, name="xs%d" % b, align_bytes=64)
+
+        def mask(u):
+            t = er[u]
+            for T in range(4):
+                blk = t[:, T, T * P:(T + 1) * P]
+                nc.vector.tensor_tensor(out=blk, in0=blk, in1=offd[:], op=ALU.mult)
+
+        def norm(u):
+            t = er[u]
+            ssum = small.tile([P, 4], F32, name="ssum")
+            for T in range(4):
+                nc.scalar.activation(out=junk[:], in_=t[:, T, :], func=ACT.Abs, accum_out=ssum[:, T:T + 1])
+            if u == NU - 1:
+                nc.scalar.activation(out=junk1[:], in_=ssum[:, 3:4], func=ACT.Sqrt)
+            rs = small.tile([P, 4], F32, name="rs")
+            nc.vector.tensor_scalar(out=rs[:], in0=ssum[:], scalar1=EPS_L1, scalar2=None, op0=ALU.max)
+            nc.vector.reciprocal(out=rs[:], in_=rs[:])
+            for T in range(4):
+                nc.vector.tensor_scalar(out=t[:, T, :], in0=t[:, T, :], scalar1=rs[:, T:T + 1], scalar2=None, op0=ALU.mult)
+
+        def e_tr(u):
+            t = er[u]
+            eg = work.tile([P, N, 4], BF16, name="eg", align_bytes=64)
+            for h in range(2):
+                pt = tp.tile([P, 2, 4, P], BF16, name="pt", tag="tp")
+                for Th in range(2):
+                    for k in range(4):
+                        nc.tensor.transpose(pt[:, Th, k, :], t[:, 2 * h + Th, k * P:(k + 1) * P], ident_bf[:])
+                dst = eg[:, 256 * h:256 * (h + 1), :].rearrange("p (T n) k -> p T n k", T=2)
+                copy_on(EE_ENGINE[u][h], dst, pt[:].rearrange("p T k n -> p T n k"))
+            ec = work.tile([P, N], U32, name="ec", align_bytes=64)
+            es = work.tile([P, N], U8, name="es", align_bytes=64)
+            nc.vector.quantize_mx(out=ec[:].bitcast(FP8X4), scales=es[:], in_=eg[:].rearrange("p n k -> p (n k)"))
+            ecs[u] = (ec, es)
+
+        def stage1(u):
+            b = u // 2
+            ec, es = ecs[u]
+            xg = work.tile([P, N, 4], BF16, name="xg", align_bytes=64)
+            for c in range(4):
+                cols = slice(c * P, (c + 1) * P)
+                ap = mm.tile([P, 4, P], F32, name="ap", tag="mm")
+                for k in range(4):
+                    fc = slice(k * P, (k + 1) * P)
+                    nc.tensor.matmul_mx(
+                        out=ap[:, k, :],
+                        lhsT=pc[b][:, fc].bitcast(FP8X4),
+                        lhsT_scale=ps[b][:, fc],
+                        rhs=ec[:, cols].bitcast(FP8X4),
+                        rhs_scale=es[:, cols],
+                        start=True,
+                        stop=True,
+                    )
+                nc.scalar.copy(out=xg[:, cols, :], in_=ap[:].rearrange("p k n -> p n k"))
+            nc.vector.quantize_mx(out=xc[b][:, u % 2, :].bitcast(FP8X4), scales=xs[b][:, u % 2, :], in_=xg[:].rearrange("p n k -> p (n k)"))
+
+        wg = keep.tile([P, 2 * C * 4], BF16, name="wg", align_bytes=64)
+        wc = keep.tile([P, 2, C], U32, name="wc", align_bytes=64)
+        ws = keep.tile([P, 2, C], U8, name="ws", align_bytes=64)
+
+        def w_prep(g):
+            wg32 = wg[:].bitcast(F32).rearrange("p (g o u) -> p g o u", g=2, u=2)
+            for Oh in range(4):
+                wt = tp.tile([P, 2, 2, P], F32, name="wt", tag="tp")
+                for s in range(2):
+                    w32 = wr[:, 2 * Oh + s, :].bitcast(F32)
+                    for u in range(2):
+                        lo = 256 * g + P * u
+                        nc.tensor.transpose(wt[:, s, u, :], w32[:, lo:lo + P], ident_f[:])
+                dst = wg32[:, g, 256 * Oh:256 * (Oh + 1), :].rearrange("p (s o) u -> p s o u", s=2)
+                copy_on("S", dst, wt[:].rearrange("p s u o -> p s o u"))
+            nc.vector.quantize_mx(out=wc[:, g, :].bitcast(FP8X4), scales=ws[:, g, :], in_=wg[:, g * 4 * C:(g + 1) * 4 * C])
+
+        def z_bank(O, b):
+            z = mm.tile([P, N], F32, name="z", tag="mm")
+            oc = slice(O * P, (O + 1) * P)
+            for g in range(2):
+                nc.tensor.matmul_mx(
+                    out=z[:],
+                    lhsT=wc[:, g, oc].bitcast(FP8X4),
+                    lhsT_scale=ws[:, g, oc],
+                    rhs=xc[b][:, g, :].bitcast(FP8X4),
+                    rhs_scale=xs[b][:, g, :],
+                    start=(g == 0),
+                    stop=(g == 1),
+                )
+            return z
+
+        def stats(b, O):
+            z = z_bank(O, b)
+            nc.vector.bn_stats(out=st[:, O, b, :], in_=z[:])
+
+        mv = const.tile([P, NO, 2], F32, name="mv")
+        sd = const.tile([P, NO], F32, name="sd")
+        rstd = const.tile([P, NO], F32, name="rstd")
+        ca = const.tile([P, NO], F32, name="ca")
+        cm = const.tile([P, NO], F32, name="cm")
+        cb = const.tile([P, NO], F32, name="cb")
+
+        def coeffs(lo, hi):
+            for O in range(lo, hi):
+                nc.vector.bn_aggr(out=mv[:, O, :], in_=st[:, O, :, :].rearrange("p b s -> p (b s)"))
+            nc.scalar.activation(out=sd[:, lo:hi], in_=mv[:, lo:hi, 1], func=ACT.Sqrt, bias=eps_t[:, 0:1], scale=1.0)
+            nc.vector.reciprocal(out=rstd[:, lo:hi], in_=sd[:, lo:hi])
+            nc.vector.tensor_tensor(out=ca[:, lo:hi], in0=rstd[:, lo:hi], in1=gbT[:, lo:hi], op=ALU.mult)
+            nc.vector.tensor_tensor(out=cm[:, lo:hi], in0=mv[:, lo:hi, 0], in1=ca[:, lo:hi], op=ALU.mult)
+            nc.vector.tensor_tensor(out=cb[:, lo:hi], in0=gbT[:, NO + lo:NO + hi], in1=cm[:, lo:hi], op=ALU.subtract)
+
+        out_view = out.rearrange("b (O p) n -> O p b n", p=P)
+
+        def final(O):
+            y = ypool.tile([P, B, N], F32, name="y")
+            yo = ypool.tile([P, B, N], F32, name="yo", bufs=3)
+            for b in range(B):
+                z = z_bank(O, b)
+                if (O, b) in AFFINE_ON_VECTOR:
+                    nc.vector.tensor_scalar(out=y[:, b, :], in0=z[:], scalar1=ca[:, O:O + 1], scalar2=cb[:, O:O + 1], op0=ALU.mult, op1=ALU.add)
+                else:
+                    nc.scalar.activation(out=y[:, b, :], in_=z[:], func=ACT.Identity, bias=cb[:, O:O + 1], scale=ca[:, O:O + 1])
+            pieces = 2 if O == NO - 1 else 1
+            step = B // pieces
+            for i in range(pieces):
+                bs = slice(i * step, (i + 1) * step)
+                yf = y[:, bs, :].rearrange("p b n -> p (b n)")
+                nc.vector.scalar_tensor_tensor(out=yo[:, bs, :].rearrange("p b n -> p (b n)"), in0=yf, scalar=NEG_SLOPE, in1=yf, op0=ALU.mult, op1=ALU.max)
+                nc.sync.dma_start(out=out_view[O][:, bs, :], in_=yo[:, bs, :])
+
+        for k in range(-2, NU + 4):
+            if 0 <= k - 1 < NU:
+                stage1(k - 1)
+            for b in range(B):
+                for O in range(NO):
+                    if 2 * b + 3 + O // 4 == k:
+                        stats(b, O)
+            if k == NU + 1:
+                coeffs(0, 4)
+            if 0 <= k < NU:
+                e_tr(k)
+            if k % 2 == 1 and 0 <= k + 1 < NU:
+                pn_prep((k + 1) // 2)
+            if k in (1, 2):
+                w_prep(k - 1)
+            if 0 <= k + 2 < NU:
+                mask(k + 2)
+            if 0 <= k + 1 < NU:
+                norm(k + 1)
+        coeffs(4, 8)
+        for O in range(NO):
+            final(O)
+
+
+EE_ENGINE = (("V", "V"), ("V", "V"), ("S", "V"), ("S", "V"), ("S", "V"), ("S", "S"), ("S", "S"), ("S", "S"))
+AFFINE_ON_VECTOR = ((0, 3), (3, 3), (6, 3))

@@ -33,10 +33,10 @@ def tile_yuyipointupdate_pa_kernel(tc, distribution_edge, instance_edge, point_n
         raw = ctx.enter_context(tc.tile_pool(name="raw", bufs=1))
         keep = ctx.enter_context(tc.tile_pool(name="keep", bufs=1))
         work = ctx.enter_context(tc.tile_pool(name="work", bufs=3))
-        small = ctx.enter_context(tc.tile_pool(name="small", bufs=4))
-        ypool = ctx.enter_context(tc.tile_pool(name="ypool", bufs=2))
+        ypool = ctx.enter_context(tc.tile_pool(name="ypool", bufs=3))
         tp = ctx.enter_context(tc.psum_pool(name="tp", bufs=3))
         mm = ctx.enter_context(tc.psum_pool(name="mm", bufs=5))
+        ctx.enter_context(tc.manual_schedule())
 
         er = {}
         pr = {}
@@ -79,108 +79,37 @@ def tile_yuyipointupdate_pa_kernel(tc, distribution_edge, instance_edge, point_n
         junk = const.tile([P, N], BF16, name="junk")
         junk1 = const.tile([P, 1], F32, name="junk1")
         st = const.tile([P, NO, B, 6], F32, name="st")
+        ssum = const.tile([P, NU, 8], F32, name="ssum")
+        rs = const.tile([P, NU, 8], F32, name="rs")
 
         gps = tp.tile([P, P], BF16, name="gps", tag="tp")
         nc.tensor.transpose(gps[:], gb[:], ident_bf[:])
         gbT = const.tile([P, 2 * NO], F32, name="gbT")
         nc.vector.tensor_copy(out=gbT[:], in_=gps[:, 0:2 * NO])
 
+        wg = keep.tile([P, 2 * C * 4], BF16, name="wg", align_bytes=64)
+        wc = keep.tile([P, 2, C], U32, name="wc", align_bytes=64)
+        ws = keep.tile([P, 2, C], U8, name="ws", align_bytes=64)
+        wg32 = wg[:].bitcast(F32).rearrange("p (g o u) -> p g o u", g=2, u=2)
+        mv = const.tile([P, NO, 2], F32, name="mv")
+        sd = const.tile([P, NO], F32, name="sd")
+        rstd = const.tile([P, NO], F32, name="rstd")
+        ca = const.tile([P, NO], F32, name="ca")
+        cm = const.tile([P, NO], F32, name="cm")
+        cb = const.tile([P, NO], F32, name="cb")
+        out_view = out.rearrange("b (O p) n -> O p b n", p=P)
+
         pc = {}
         ps = {}
         xc = {}
         xs = {}
-        ecs = {}
-        rss = {}
+        live = {}
 
         def copy_on(engine, dst, src):
             if engine == "S":
                 nc.scalar.copy(out=dst, in_=src)
             else:
                 nc.vector.tensor_copy(out=dst, in_=src)
-
-        def pn_prep(b):
-            png = work.tile([P, D, 4], BF16, name="png", align_bytes=64, bufs=2)
-            dst = png[:].rearrange("q (u e p) t -> q u e p t", u=2, e=2)
-            src = pr[b][:].rearrange("q t (u p e) -> q u e p t", u=2, e=2)
-            for u in range(2):
-                nc.vector.tensor_copy(out=dst[:, u], in_=src[:, u])
-            pc[b] = keep.tile([P, D], U32, name="pc%d" % b, align_bytes=64)
-            ps[b] = keep.tile([P, D], U8, name="ps%d" % b, align_bytes=64)
-            nc.vector.quantize_mx(out=pc[b][:].bitcast(FP8X4), scales=ps[b][:], in_=png[:].rearrange("q c t -> q (c t)"))
-            xc[b] = keep.tile([P, 2, N], U32, name="xc%d" % b, align_bytes=64)
-            xs[b] = keep.tile([P, 2, N], U8, name="xs%d" % b, align_bytes=64)
-
-        def mask(u):
-            t = er[u]
-            for T in range(4):
-                blk = t[:, T, T * P:(T + 1) * P]
-                nc.vector.tensor_tensor(out=blk, in0=blk, in1=offd[:], op=ALU.mult)
-
-        def norm(u):
-            t = er[u]
-            ssum = small.tile([P, 4], F32, name="ssum")
-            for T in range(4):
-                nc.scalar.activation(out=junk[:], in_=t[:, T, :], func=ACT.Abs, accum_out=ssum[:, T:T + 1])
-            if u == NU - 1:
-                nc.scalar.activation(out=junk1[:], in_=ssum[:, 3:4], func=ACT.Sqrt)
-            rs = small.tile([P, 4], F32, name="rs")
-            nc.vector.tensor_scalar(out=rs[:], in0=ssum[:], scalar1=EPS_L1, scalar2=None, op0=ALU.max)
-            nc.vector.reciprocal(out=rs[:], in_=rs[:])
-            for T in range(4):
-                nc.vector.tensor_scalar(out=t[:, T, :], in0=t[:, T, :], scalar1=rs[:, T:T + 1], scalar2=None, op0=ALU.mult)
-
-        def e_tr(u):
-            t = er[u]
-            eg = work.tile([P, N, 4], BF16, name="eg", align_bytes=64)
-            for h in range(2):
-                pt = tp.tile([P, 2, 4, P], BF16, name="pt", tag="tp")
-                for Th in range(2):
-                    for k in range(4):
-                        nc.tensor.transpose(pt[:, Th, k, :], t[:, 2 * h + Th, k * P:(k + 1) * P], ident_bf[:])
-                dst = eg[:, 256 * h:256 * (h + 1), :].rearrange("p (T n) k -> p T n k", T=2)
-                copy_on(EE_ENGINE[u][h], dst, pt[:].rearrange("p T k n -> p T n k"))
-            ec = work.tile([P, N], U32, name="ec", align_bytes=64)
-            es = work.tile([P, N], U8, name="es", align_bytes=64)
-            nc.vector.quantize_mx(out=ec[:].bitcast(FP8X4), scales=es[:], in_=eg[:].rearrange("p n k -> p (n k)"))
-            ecs[u] = (ec, es)
-
-        def stage1(u):
-            b = u // 2
-            ec, es = ecs[u]
-            xg = work.tile([P, N, 4], BF16, name="xg", align_bytes=64)
-            for c in range(4):
-                cols = slice(c * P, (c + 1) * P)
-                ap = mm.tile([P, 4, P], F32, name="ap", tag="mm")
-                for k in range(4):
-                    fc = slice(k * P, (k + 1) * P)
-                    nc.tensor.matmul_mx(
-                        out=ap[:, k, :],
-                        lhsT=pc[b][:, fc].bitcast(FP8X4),
-                        lhsT_scale=ps[b][:, fc],
-                        rhs=ec[:, cols].bitcast(FP8X4),
-                        rhs_scale=es[:, cols],
-                        start=True,
-                        stop=True,
-                    )
-                nc.scalar.copy(out=xg[:, cols, :], in_=ap[:].rearrange("p k n -> p n k"))
-            nc.vector.quantize_mx(out=xc[b][:, u % 2, :].bitcast(FP8X4), scales=xs[b][:, u % 2, :], in_=xg[:].rearrange("p n k -> p (n k)"))
-
-        wg = keep.tile([P, 2 * C * 4], BF16, name="wg", align_bytes=64)
-        wc = keep.tile([P, 2, C], U32, name="wc", align_bytes=64)
-        ws = keep.tile([P, 2, C], U8, name="ws", align_bytes=64)
-
-        def w_prep(g):
-            wg32 = wg[:].bitcast(F32).rearrange("p (g o u) -> p g o u", g=2, u=2)
-            for Oh in range(4):
-                wt = tp.tile([P, 2, 2, P], F32, name="wt", tag="tp")
-                for s in range(2):
-                    w32 = wr[:, 2 * Oh + s, :].bitcast(F32)
-                    for u in range(2):
-                        lo = 256 * g + P * u
-                        nc.tensor.transpose(wt[:, s, u, :], w32[:, lo:lo + P], ident_f[:])
-                dst = wg32[:, g, 256 * Oh:256 * (Oh + 1), :].rearrange("p (s o) u -> p s o u", s=2)
-                copy_on("S", dst, wt[:].rearrange("p s u o -> p s o u"))
-            nc.vector.quantize_mx(out=wc[:, g, :].bitcast(FP8X4), scales=ws[:, g, :], in_=wg[:, g * 4 * C:(g + 1) * 4 * C])
 
         def z_bank(O, b):
             z = mm.tile([P, N], F32, name="z", tag="mm")
@@ -197,68 +126,180 @@ def tile_yuyipointupdate_pa_kernel(tc, distribution_edge, instance_edge, point_n
                 )
             return z
 
-        def stats(b, O):
-            z = z_bank(O, b)
-            nc.vector.bn_stats(out=st[:, O, b, :], in_=z[:])
-
-        mv = const.tile([P, NO, 2], F32, name="mv")
-        sd = const.tile([P, NO], F32, name="sd")
-        rstd = const.tile([P, NO], F32, name="rstd")
-        ca = const.tile([P, NO], F32, name="ca")
-        cm = const.tile([P, NO], F32, name="cm")
-        cb = const.tile([P, NO], F32, name="cb")
-
-        def coeffs(lo, hi):
-            for O in range(lo, hi):
-                nc.vector.bn_aggr(out=mv[:, O, :], in_=st[:, O, :, :].rearrange("p b s -> p (b s)"))
-            nc.scalar.activation(out=sd[:, lo:hi], in_=mv[:, lo:hi, 1], func=ACT.Sqrt, bias=eps_t[:, 0:1], scale=1.0)
-            nc.vector.reciprocal(out=rstd[:, lo:hi], in_=sd[:, lo:hi])
-            nc.vector.tensor_tensor(out=ca[:, lo:hi], in0=rstd[:, lo:hi], in1=gbT[:, lo:hi], op=ALU.mult)
-            nc.vector.tensor_tensor(out=cm[:, lo:hi], in0=mv[:, lo:hi, 0], in1=ca[:, lo:hi], op=ALU.mult)
-            nc.vector.tensor_tensor(out=cb[:, lo:hi], in0=gbT[:, NO + lo:NO + hi], in1=cm[:, lo:hi], op=ALU.subtract)
-
-        out_view = out.rearrange("b (O p) n -> O p b n", p=P)
-
-        def final(O):
-            y = ypool.tile([P, B, N], F32, name="y")
-            yo = ypool.tile([P, B, N], F32, name="yo", bufs=3)
-            for b in range(B):
-                z = z_bank(O, b)
-                if (O, b) in AFFINE_ON_VECTOR:
-                    nc.vector.tensor_scalar(out=y[:, b, :], in0=z[:], scalar1=ca[:, O:O + 1], scalar2=cb[:, O:O + 1], op0=ALU.mult, op1=ALU.add)
+        def step(kind, i, j, engine):
+            if kind == "mk":
+                t = er[i]
+                for T in range(4):
+                    blk = t[:, T, T * P:(T + 1) * P]
+                    nc.vector.tensor_tensor(out=blk, in0=blk, in1=offd[:], op=ALU.mult)
+            elif kind == "ab":
+                for T in range(4):
+                    nc.scalar.activation(out=junk[:], in_=er[i][:, T, :], func=ACT.Abs, accum_out=ssum[:, i, T:T + 1])
+                if i == NU - 1:
+                    nc.scalar.activation(out=junk1[:], in_=ssum[:, i, 3:4], func=ACT.Sqrt)
+            elif kind == "sc":
+                nc.vector.tensor_scalar(out=rs[:, i, 0:4], in0=ssum[:, i, 0:4], scalar1=EPS_L1, scalar2=None, op0=ALU.max)
+                nc.vector.reciprocal(out=rs[:, i, 0:4], in_=rs[:, i, 0:4])
+                for T in range(4):
+                    nc.vector.tensor_scalar(out=er[i][:, T, :], in0=er[i][:, T, :], scalar1=rs[:, i, T:T + 1], scalar2=None, op0=ALU.mult)
+            elif kind == "tr":
+                pt = tp.tile([P, 2, 4, P], BF16, name="pt", tag="tp")
+                for Th in range(2):
+                    for k in range(4):
+                        nc.tensor.transpose(pt[:, Th, k, :], er[i][:, 2 * j + Th, k * P:(k + 1) * P], ident_bf[:])
+                live[("pt", i, j)] = pt
+            elif kind == "ee":
+                if ("eg", i) not in live:
+                    live[("eg", i)] = work.tile([P, N, 4], BF16, name="eg", align_bytes=64)
+                dst = live[("eg", i)][:, 256 * j:256 * (j + 1), :].rearrange("p (T n) k -> p T n k", T=2)
+                copy_on(engine, dst, live[("pt", i, j)][:].rearrange("p T k n -> p T n k"))
+            elif kind == "qe":
+                ec = work.tile([P, N], U32, name="ec", align_bytes=64)
+                es = work.tile([P, N], U8, name="es", align_bytes=64)
+                nc.vector.quantize_mx(out=ec[:].bitcast(FP8X4), scales=es[:], in_=live[("eg", i)][:].rearrange("p n k -> p (n k)"))
+                live[("ec", i)] = (ec, es)
+            elif kind == "pr":
+                png = work.tile([P, D, 4], BF16, name="png", align_bytes=64, bufs=2)
+                dst = png[:].rearrange("q (u e p) t -> q u e p t", u=2, e=2)
+                src = pr[i][:].rearrange("q t (u p e) -> q u e p t", u=2, e=2)
+                for u in range(2):
+                    nc.vector.tensor_copy(out=dst[:, u], in_=src[:, u])
+                live[("png", i)] = png
+            elif kind == "qp":
+                pc[i] = keep.tile([P, D], U32, name="pc%d" % i, align_bytes=64)
+                ps[i] = keep.tile([P, D], U8, name="ps%d" % i, align_bytes=64)
+                nc.vector.quantize_mx(out=pc[i][:].bitcast(FP8X4), scales=ps[i][:], in_=live[("png", i)][:].rearrange("q c t -> q (c t)"))
+                xc[i] = keep.tile([P, 2, N], U32, name="xc%d" % i, align_bytes=64)
+                xs[i] = keep.tile([P, 2, N], U8, name="xs%d" % i, align_bytes=64)
+            elif kind == "m":
+                b = i // 2
+                ec, es = live[("ec", i)]
+                cols = slice(j * P, (j + 1) * P)
+                ap = mm.tile([P, 4, P], F32, name="ap", tag="mm")
+                for k in range(4):
+                    fc = slice(k * P, (k + 1) * P)
+                    nc.tensor.matmul_mx(
+                        out=ap[:, k, :],
+                        lhsT=pc[b][:, fc].bitcast(FP8X4),
+                        lhsT_scale=ps[b][:, fc],
+                        rhs=ec[:, cols].bitcast(FP8X4),
+                        rhs_scale=es[:, cols],
+                        start=True,
+                        stop=True,
+                    )
+                live[("ap", i, j)] = ap
+            elif kind == "ex":
+                if ("xg", i) not in live:
+                    live[("xg", i)] = work.tile([P, N, 4], BF16, name="xg", align_bytes=64)
+                copy_on(engine, live[("xg", i)][:, j * P:(j + 1) * P, :], live[("ap", i, j)][:].rearrange("p k n -> p n k"))
+            elif kind == "qx":
+                b = i // 2
+                nc.vector.quantize_mx(out=xc[b][:, i % 2, :].bitcast(FP8X4), scales=xs[b][:, i % 2, :], in_=live[("xg", i)][:].rearrange("p n k -> p (n k)"))
+            elif kind == "wt":
+                wt = tp.tile([P, 2, 2, P], F32, name="wt", tag="tp")
+                for s in range(2):
+                    w32 = wr[:, 2 * j + s, :].bitcast(F32)
+                    for u in range(2):
+                        lo = 256 * i + P * u
+                        nc.tensor.transpose(wt[:, s, u, :], w32[:, lo:lo + P], ident_f[:])
+                live[("wt", i, j)] = wt
+            elif kind == "we":
+                dst = wg32[:, i, 256 * j:256 * (j + 1), :].rearrange("p (s o) u -> p s o u", s=2)
+                copy_on(engine, dst, live[("wt", i, j)][:].rearrange("p s u o -> p s o u"))
+            elif kind == "qw":
+                nc.vector.quantize_mx(out=wc[:, i, :].bitcast(FP8X4), scales=ws[:, i, :], in_=wg[:, i * 4 * C:(i + 1) * 4 * C])
+            elif kind == "z":
+                live[("z", i, j)] = z_bank(j, i)
+            elif kind == "bn":
+                nc.vector.bn_stats(out=st[:, j, i, :], in_=live[("z", i, j)][:])
+            elif kind == "ag":
+                for O in range(4 * i, 4 * i + 4):
+                    nc.vector.bn_aggr(out=mv[:, O, :], in_=st[:, O, :, :].rearrange("p b s -> p (b s)"))
+            elif kind == "sq":
+                lo, hi = 4 * i, 4 * i + 4
+                nc.scalar.activation(out=sd[:, lo:hi], in_=mv[:, lo:hi, 1], func=ACT.Sqrt, bias=eps_t[:, 0:1], scale=1.0)
+            elif kind == "co":
+                lo, hi = 4 * i, 4 * i + 4
+                nc.vector.reciprocal(out=rstd[:, lo:hi], in_=sd[:, lo:hi])
+                nc.vector.tensor_tensor(out=ca[:, lo:hi], in0=rstd[:, lo:hi], in1=gbT[:, lo:hi], op=ALU.mult)
+                nc.vector.tensor_tensor(out=cm[:, lo:hi], in0=mv[:, lo:hi, 0], in1=ca[:, lo:hi], op=ALU.mult)
+                nc.vector.tensor_tensor(out=cb[:, lo:hi], in0=gbT[:, NO + lo:NO + hi], in1=cm[:, lo:hi], op=ALU.subtract)
+            elif kind == "f":
+                live[("f", i, j)] = z_bank(i, j)
+            elif kind == "af":
+                if ("y", i) not in live:
+                    live[("y", i)] = ypool.tile([P, B, N], F32, name="y")
+                y = live[("y", i)]
+                z = live[("f", i, j)]
+                if engine == "V":
+                    nc.vector.tensor_scalar(out=y[:, j, :], in0=z[:], scalar1=ca[:, i:i + 1], scalar2=cb[:, i:i + 1], op0=ALU.mult, op1=ALU.add)
                 else:
-                    nc.scalar.activation(out=y[:, b, :], in_=z[:], func=ACT.Identity, bias=cb[:, O:O + 1], scale=ca[:, O:O + 1])
-            pieces = 2 if O == NO - 1 else 1
-            step = B // pieces
-            for i in range(pieces):
-                bs = slice(i * step, (i + 1) * step)
-                yf = y[:, bs, :].rearrange("p b n -> p (b n)")
-                nc.vector.scalar_tensor_tensor(out=yo[:, bs, :].rearrange("p b n -> p (b n)"), in0=yf, scalar=NEG_SLOPE, in1=yf, op0=ALU.mult, op1=ALU.max)
-                nc.sync.dma_start(out=out_view[O][:, bs, :], in_=yo[:, bs, :])
+                    nc.scalar.activation(out=y[:, j, :], in_=z[:], func=ACT.Identity, bias=cb[:, i:i + 1], scale=ca[:, i:i + 1])
+            elif kind == "lr":
+                y = live[("y", i)]
+                yo = ypool.tile([P, B, N], F32, name="yo")
+                pieces = 2 if i == NO - 1 else 1
+                width = B // pieces
+                for q in range(pieces):
+                    bs = slice(q * width, (q + 1) * width)
+                    yf = y[:, bs, :].rearrange("p b n -> p (b n)")
+                    nc.vector.scalar_tensor_tensor(out=yo[:, bs, :].rearrange("p b n -> p (b n)"), in0=yf, scalar=NEG_SLOPE, in1=yf, op0=ALU.mult, op1=ALU.max)
+                    nc.sync.dma_start(out=out_view[i][:, bs, :], in_=yo[:, bs, :])
 
-        for k in range(-2, NU + 4):
-            if 0 <= k - 1 < NU:
-                stage1(k - 1)
-            for b in range(B):
-                for O in range(NO):
-                    if 2 * b + 3 + O // 4 == k:
-                        stats(b, O)
-            if k == NU + 1:
-                coeffs(0, 4)
-            if 0 <= k < NU:
-                e_tr(k)
-            if k % 2 == 1 and 0 <= k + 1 < NU:
-                pn_prep((k + 1) // 2)
-            if k in (1, 2):
-                w_prep(k - 1)
-            if 0 <= k + 2 < NU:
-                mask(k + 2)
-            if 0 <= k + 1 < NU:
-                norm(k + 1)
-        coeffs(4, 8)
-        for O in range(NO):
-            final(O)
+        for kind, i, j, engine in ORDER:
+            step(kind, i, j, engine)
 
 
-EE_ENGINE = (("V", "V"), ("V", "V"), ("S", "V"), ("S", "V"), ("S", "V"), ("S", "S"), ("S", "S"), ("S", "S"))
-AFFINE_ON_VECTOR = ((0, 3), (3, 3), (6, 3))
+ORDER = (
+    ("mk", 0, 0, "V"), ("ab", 0, 0, "S"), ("pr", 0, 0, "V"), ("qp", 0, 0, "V"), ("mk", 1, 0, "V"), ("sc", 0, 0, "V"),
+    ("ab", 1, 0, "S"), ("wt", 0, 0, "PE"), ("wt", 0, 1, "PE"), ("tr", 0, 0, "PE"), ("we", 0, 0, "S"), ("ee", 0, 0, "V"),
+    ("we", 0, 1, "S"), ("tr", 0, 1, "PE"), ("sc", 1, 0, "V"), ("wt", 0, 2, "PE"), ("wt", 0, 3, "PE"), ("ee", 0, 1, "V"),
+    ("we", 0, 2, "S"), ("we", 0, 3, "S"), ("qe", 0, 0, "V"), ("tr", 1, 0, "PE"), ("mk", 2, 0, "V"), ("tr", 1, 1, "PE"),
+    ("pr", 1, 0, "V"), ("ab", 2, 0, "S"), ("m", 0, 0, "PE"), ("m", 0, 1, "PE"), ("m", 0, 2, "PE"), ("ee", 1, 0, "V"),
+    ("m", 0, 3, "PE"), ("wt", 1, 0, "PE"), ("ee", 1, 1, "V"), ("wt", 1, 1, "PE"), ("ex", 0, 0, "S"), ("qe", 1, 0, "V"),
+    ("ex", 0, 1, "S"), ("wt", 1, 2, "PE"), ("qp", 1, 0, "V"), ("ex", 0, 2, "S"), ("m", 1, 0, "PE"), ("qw", 0, 0, "V"),
+    ("ex", 0, 3, "S"), ("m", 1, 1, "PE"), ("m", 1, 2, "PE"), ("we", 1, 0, "S"), ("m", 1, 3, "PE"), ("mk", 3, 0, "V"),
+    ("ex", 1, 0, "S"), ("qx", 0, 0, "V"), ("wt", 1, 3, "PE"), ("ex", 1, 1, "S"), ("sc", 2, 0, "V"), ("ex", 1, 2, "S"),
+    ("mk", 4, 0, "V"), ("ex", 1, 3, "S"), ("pr", 2, 0, "V"), ("we", 1, 1, "S"), ("we", 1, 2, "S"), ("qx", 1, 0, "V"),
+    ("tr", 2, 0, "PE"), ("we", 1, 3, "S"), ("qp", 2, 0, "V"), ("tr", 2, 1, "PE"), ("ab", 3, 0, "S"), ("mk", 5, 0, "V"),
+    ("qw", 1, 0, "V"), ("ee", 2, 1, "V"), ("z", 0, 0, "PE"), ("ee", 2, 0, "S"), ("z", 0, 1, "PE"), ("mk", 6, 0, "V"),
+    ("sc", 3, 0, "V"), ("z", 0, 2, "PE"), ("ab", 4, 0, "S"), ("z", 0, 3, "PE"), ("qe", 2, 0, "V"), ("z", 0, 4, "PE"),
+    ("bn", 0, 0, "V"), ("tr", 3, 0, "PE"), ("bn", 0, 1, "V"), ("tr", 3, 1, "PE"), ("bn", 0, 2, "V"), ("m", 2, 0, "PE"),
+    ("ee", 3, 0, "S"), ("m", 2, 1, "PE"), ("bn", 0, 3, "V"), ("m", 2, 2, "PE"), ("ee", 3, 1, "V"), ("ex", 2, 0, "S"),
+    ("m", 2, 3, "PE"), ("ex", 2, 1, "S"), ("qe", 3, 0, "V"), ("z", 0, 5, "PE"), ("ex", 2, 2, "S"), ("sc", 4, 0, "V"),
+    ("z", 0, 6, "PE"), ("ex", 2, 3, "S"), ("m", 3, 0, "PE"), ("ab", 5, 0, "S"), ("bn", 0, 4, "V"), ("m", 3, 1, "PE"),
+    ("qx", 2, 0, "V"), ("tr", 4, 0, "PE"), ("bn", 0, 5, "V"), ("m", 3, 2, "PE"), ("tr", 4, 1, "PE"), ("bn", 0, 6, "V"),
+    ("m", 3, 3, "PE"), ("pr", 3, 0, "V"), ("ex", 3, 0, "S"), ("z", 0, 7, "PE"), ("ex", 3, 1, "S"), ("ex", 3, 2, "S"),
+    ("ee", 4, 1, "V"), ("ex", 3, 3, "S"), ("ee", 4, 0, "S"), ("bn", 0, 7, "V"), ("qx", 3, 0, "V"), ("ab", 6, 0, "S"),
+    ("sc", 5, 0, "V"), ("z", 1, 0, "PE"), ("qe", 4, 0, "V"), ("z", 1, 1, "PE"), ("bn", 1, 0, "V"), ("z", 1, 2, "PE"),
+    ("m", 4, 0, "PE"), ("bn", 1, 1, "V"), ("m", 4, 1, "PE"), ("bn", 1, 2, "V"), ("m", 4, 2, "PE"), ("ex", 4, 0, "S"),
+    ("tr", 5, 0, "PE"), ("qp", 3, 0, "V"), ("ex", 4, 1, "S"), ("m", 4, 3, "PE"), ("mk", 7, 0, "V"), ("z", 1, 3, "PE"),
+    ("ex", 4, 2, "S"), ("sc", 6, 0, "V"), ("tr", 5, 1, "PE"), ("ex", 4, 3, "S"), ("z", 1, 4, "PE"), ("bn", 1, 3, "V"),
+    ("ee", 5, 0, "S"), ("z", 1, 5, "PE"), ("qx", 4, 0, "V"), ("z", 1, 6, "PE"), ("bn", 1, 4, "V"), ("ee", 5, 1, "S"),
+    ("z", 1, 7, "PE"), ("bn", 1, 5, "V"), ("tr", 6, 0, "PE"), ("bn", 1, 6, "V"), ("ab", 7, 0, "S"), ("tr", 6, 1, "PE"),
+    ("qe", 5, 0, "V"), ("bn", 1, 7, "V"), ("m", 5, 0, "PE"), ("m", 5, 1, "PE"), ("m", 5, 2, "PE"), ("m", 5, 3, "PE"),
+    ("ex", 5, 0, "S"), ("sc", 7, 0, "V"), ("ex", 5, 1, "S"), ("ex", 5, 2, "S"), ("ex", 5, 3, "S"), ("tr", 7, 0, "PE"),
+    ("ee", 6, 0, "S"), ("qx", 5, 0, "V"), ("ee", 6, 1, "S"), ("z", 2, 0, "PE"), ("z", 2, 1, "PE"), ("ee", 7, 0, "S"),
+    ("bn", 2, 0, "V"), ("z", 2, 2, "PE"), ("qe", 6, 0, "V"), ("z", 2, 3, "PE"), ("tr", 7, 1, "PE"), ("bn", 2, 1, "V"),
+    ("m", 6, 0, "PE"), ("bn", 2, 2, "V"), ("m", 6, 1, "PE"), ("ee", 7, 1, "S"), ("m", 6, 2, "PE"), ("bn", 2, 3, "V"),
+    ("m", 6, 3, "PE"), ("ex", 6, 0, "S"), ("z", 2, 4, "PE"), ("qe", 7, 0, "V"), ("ex", 6, 1, "S"), ("z", 2, 5, "PE"),
+    ("bn", 2, 4, "V"), ("ex", 6, 2, "S"), ("m", 7, 0, "PE"), ("ex", 6, 3, "S"), ("bn", 2, 5, "V"), ("m", 7, 1, "PE"),
+    ("ex", 7, 0, "S"), ("m", 7, 2, "PE"), ("qx", 6, 0, "V"), ("m", 7, 3, "PE"), ("ex", 7, 1, "S"), ("z", 2, 6, "PE"),
+    ("ex", 7, 2, "S"), ("z", 2, 7, "PE"), ("bn", 2, 6, "V"), ("ex", 7, 3, "S"), ("bn", 2, 7, "V"), ("qx", 7, 0, "V"),
+    ("z", 3, 0, "PE"), ("z", 3, 1, "PE"), ("bn", 3, 0, "V"), ("z", 3, 2, "PE"), ("bn", 3, 1, "V"), ("z", 3, 3, "PE"),
+    ("z", 3, 4, "PE"), ("bn", 3, 2, "V"), ("z", 3, 5, "PE"), ("bn", 3, 3, "V"), ("z", 3, 6, "PE"), ("bn", 3, 4, "V"),
+    ("z", 3, 7, "PE"), ("bn", 3, 5, "V"), ("bn", 3, 6, "V"), ("bn", 3, 7, "V"), ("ag", 0, 0, "V"), ("ag", 1, 0, "V"),
+    ("sq", 0, 0, "S"), ("sq", 1, 0, "S"), ("co", 0, 0, "V"), ("co", 1, 0, "V"), ("f", 0, 0, "PE"), ("f", 0, 1, "PE"),
+    ("af", 0, 0, "S"), ("f", 0, 2, "PE"), ("f", 0, 3, "PE"), ("af", 0, 1, "S"), ("f", 1, 0, "PE"), ("af", 0, 2, "S"),
+    ("af", 0, 3, "V"), ("f", 1, 1, "PE"), ("af", 1, 0, "S"), ("f", 1, 2, "PE"), ("lr", 0, 0, "V"), ("f", 1, 3, "PE"),
+    ("af", 1, 1, "S"), ("f", 2, 0, "PE"), ("af", 1, 2, "S"), ("f", 2, 1, "PE"), ("af", 1, 3, "S"), ("f", 2, 2, "PE"),
+    ("af", 2, 0, "S"), ("f", 2, 3, "PE"), ("lr", 1, 0, "V"), ("af", 2, 1, "S"), ("f", 3, 0, "PE"), ("f", 3, 1, "PE"),
+    ("af", 2, 2, "S"), ("f", 3, 2, "PE"), ("af", 2, 3, "S"), ("f", 3, 3, "PE"), ("af", 3, 0, "S"), ("lr", 2, 0, "V"),
+    ("f", 4, 0, "PE"), ("af", 3, 1, "S"), ("f", 4, 1, "PE"), ("af", 3, 2, "S"), ("f", 4, 2, "PE"), ("af", 4, 0, "S"),
+    ("f", 4, 3, "PE"), ("af", 4, 1, "S"), ("af", 3, 3, "V"), ("f", 5, 0, "PE"), ("af", 4, 2, "S"), ("lr", 3, 0, "V"),
+    ("f", 5, 1, "PE"), ("af", 4, 3, "S"), ("f", 5, 2, "PE"), ("af", 5, 0, "S"), ("f", 5, 3, "PE"), ("af", 5, 1, "S"),
+    ("f", 6, 0, "PE"), ("lr", 4, 0, "V"), ("af", 5, 2, "S"), ("f", 6, 1, "PE"), ("f", 6, 2, "PE"), ("af", 5, 3, "S"),
+    ("f", 6, 3, "PE"), ("af", 6, 0, "S"), ("lr", 5, 0, "V"), ("f", 7, 0, "PE"), ("af", 6, 1, "S"), ("f", 7, 1, "PE"),
+    ("af", 6, 2, "S"), ("f", 7, 2, "PE"), ("af", 7, 0, "S"), ("f", 7, 3, "PE"), ("af", 7, 1, "S"), ("af", 6, 3, "V"),
+    ("af", 7, 2, "S"), ("lr", 6, 0, "V"), ("af", 7, 3, "S"), ("lr", 7, 0, "V"),
+)

@@ -18,6 +18,7 @@ D = 512
 C = 1024
 NO = C // P
 NU = 2 * B
+GRP = 2
 EPS_L1 = 1e-12
 EPS_BN = 1e-5
 NEG_SLOPE = 0.01
@@ -34,39 +35,38 @@ def tile_yuyipointupdate_pa_kernel(tc, distribution_edge, instance_edge, point_n
         keep = ctx.enter_context(tc.tile_pool(name="keep", bufs=1))
         work = ctx.enter_context(tc.tile_pool(name="work", bufs=3))
         ypool = ctx.enter_context(tc.tile_pool(name="ypool", bufs=3))
-        tp = ctx.enter_context(tc.psum_pool(name="tp", bufs=3))
-        mm = ctx.enter_context(tc.psum_pool(name="mm", bufs=5))
+        psum = ctx.enter_context(tc.psum_pool(name="psum", bufs=8))
         ctx.enter_context(tc.manual_schedule())
 
         er = {}
+        er3 = {}
         pr = {}
-
-        def load_edge(u):
-            t = raw.tile([P, 4, N], BF16, name="er%d" % u)
-            nc.sync.dma_start(out=t[:], in_=edges[u % 2][u // 2].rearrange("(T p) m -> p T m", p=P))
-            er[u] = t
-
-        def load_pn(b):
-            t = raw.tile([P, 4, D], BF16, name="pr%d" % b)
-            nc.sync.dma_start(out=t[:], in_=point_node[b].rearrange("(t p) f -> p t f", p=P))
-            pr[b] = t
 
         gb = const.tile([P, P], BF16, name="gb")
         nc.vector.memset(gb[:], 0.0)
         nc.scalar.dma_start(out=gb[0:NO, :], in_=g1.rearrange("(o p) -> o p", p=P))
         nc.scalar.dma_start(out=gb[NO:2 * NO, :], in_=b1.rearrange("(o p) -> o p", p=P))
 
-        load_edge(0)
-        load_pn(0)
-        load_edge(1)
         wr = raw.tile([P, NO, C], BF16, name="wr")
         w_view = W1.rearrange("(O p) c -> p O c", p=P)
-        nc.sync.dma_start(out=wr[:, 0:4, :], in_=w_view[:, 0:4, :])
-        nc.sync.dma_start(out=wr[:, 4:8, :], in_=w_view[:, 4:8, :])
-        for b in range(1, B):
-            load_edge(2 * b)
-            load_pn(b)
-            load_edge(2 * b + 1)
+        for what in ("E0", "P0", "E1", "E2", "W0", "E3", "P1", "W1", "E4", "P2", "E5", "E6", "P3", "E7"):
+            i = int(what[1])
+            if what[0] == "E":
+                t = raw.tile([P, 5 * N], BF16, name="er%d" % i)
+                er[i] = t
+                er3[i] = t[:, 0:4 * N].rearrange("p (T m) -> p T m", T=4)
+                src = edges[i % 2][i // 2].rearrange("(T p) m -> p T m", p=P)
+                if i == 0:
+                    nc.sync.dma_start(out=er3[i][:, 0:2, :], in_=src[:, 0:2, :])
+                    nc.sync.dma_start(out=er3[i][:, 2:4, :], in_=src[:, 2:4, :])
+                else:
+                    nc.sync.dma_start(out=er3[i], in_=src)
+            elif what[0] == "P":
+                t = raw.tile([P, 4, D], BF16, name="pr%d" % i)
+                nc.sync.dma_start(out=t[:], in_=point_node[i].rearrange("(t p) f -> p t f", p=P))
+                pr[i] = t
+            else:
+                nc.sync.dma_start(out=wr[:, 4 * i:4 * i + 4, :], in_=w_view[:, 4 * i:4 * i + 4, :])
 
         ident_bf = const.tile([P, P], BF16, name="ident_bf")
         make_identity(nc, ident_bf[:])
@@ -82,10 +82,12 @@ def tile_yuyipointupdate_pa_kernel(tc, distribution_edge, instance_edge, point_n
         ssum = const.tile([P, NU, 8], F32, name="ssum")
         rs = const.tile([P, NU, 8], F32, name="rs")
 
-        gps = tp.tile([P, P], BF16, name="gps", tag="tp")
+        gps = psum.tile([P, P], BF16, name="gps", tag="ps")
         nc.tensor.transpose(gps[:], gb[:], ident_bf[:])
-        gbT = const.tile([P, 2 * NO], F32, name="gbT")
-        nc.vector.tensor_copy(out=gbT[:], in_=gps[:, 0:2 * NO])
+        gm = const.tile([P, 2, NO], F32, name="gm")
+        nc.vector.tensor_copy(out=gm[:, 0, :], in_=gps[:, 0:NO])
+        bT = const.tile([P, NO], F32, name="bT")
+        nc.vector.tensor_copy(out=bT[:], in_=gps[:, NO:2 * NO])
 
         wg = keep.tile([P, 2 * C * 4], BF16, name="wg", align_bytes=64)
         wc = keep.tile([P, 2, C], U32, name="wc", align_bytes=64)
@@ -94,8 +96,7 @@ def tile_yuyipointupdate_pa_kernel(tc, distribution_edge, instance_edge, point_n
         mv = const.tile([P, NO, 2], F32, name="mv")
         sd = const.tile([P, NO], F32, name="sd")
         rstd = const.tile([P, NO], F32, name="rstd")
-        ca = const.tile([P, NO], F32, name="ca")
-        cm = const.tile([P, NO], F32, name="cm")
+        cc = const.tile([P, 2, NO], F32, name="cc")
         cb = const.tile([P, NO], F32, name="cb")
         out_view = out.rearrange("b (O p) n -> O p b n", p=P)
 
@@ -112,7 +113,7 @@ def tile_yuyipointupdate_pa_kernel(tc, distribution_edge, instance_edge, point_n
                 nc.vector.tensor_copy(out=dst, in_=src)
 
         def z_bank(O, b):
-            z = mm.tile([P, N], F32, name="z", tag="mm")
+            z = psum.tile([P, N], F32, name="z", tag="ps")
             oc = slice(O * P, (O + 1) * P)
             for g in range(2):
                 nc.tensor.matmul_mx(
@@ -128,25 +129,23 @@ def tile_yuyipointupdate_pa_kernel(tc, distribution_edge, instance_edge, point_n
 
         def step(kind, i, j, engine):
             if kind == "mk":
-                t = er[i]
-                for T in range(4):
-                    blk = t[:, T, T * P:(T + 1) * P]
-                    nc.vector.tensor_tensor(out=blk, in0=blk, in1=offd[:], op=ALU.mult)
+                blk = er[i][:].rearrange("p (T x) -> p T x", x=N + P)[:, :, 0:P]
+                nc.vector.tensor_tensor(out=blk, in0=blk, in1=offd[:].unsqueeze(1).to_broadcast([P, 4, P]), op=ALU.mult)
             elif kind == "ab":
                 for T in range(4):
-                    nc.scalar.activation(out=junk[:], in_=er[i][:, T, :], func=ACT.Abs, accum_out=ssum[:, i, T:T + 1])
+                    nc.scalar.activation(out=junk[:], in_=er3[i][:, T, :], func=ACT.Abs, accum_out=ssum[:, i, T:T + 1])
                 if i == NU - 1:
                     nc.scalar.activation(out=junk1[:], in_=ssum[:, i, 3:4], func=ACT.Sqrt)
             elif kind == "sc":
                 nc.vector.tensor_scalar(out=rs[:, i, 0:4], in0=ssum[:, i, 0:4], scalar1=EPS_L1, scalar2=None, op0=ALU.max)
                 nc.vector.reciprocal(out=rs[:, i, 0:4], in_=rs[:, i, 0:4])
                 for T in range(4):
-                    nc.vector.tensor_scalar(out=er[i][:, T, :], in0=er[i][:, T, :], scalar1=rs[:, i, T:T + 1], scalar2=None, op0=ALU.mult)
+                    nc.vector.tensor_scalar(out=er3[i][:, T, :], in0=er3[i][:, T, :], scalar1=rs[:, i, T:T + 1], scalar2=None, op0=ALU.mult)
             elif kind == "tr":
-                pt = tp.tile([P, 2, 4, P], BF16, name="pt", tag="tp")
+                pt = psum.tile([P, 2, 4, P], BF16, name="pt", tag="ps")
                 for Th in range(2):
                     for k in range(4):
-                        nc.tensor.transpose(pt[:, Th, k, :], er[i][:, 2 * j + Th, k * P:(k + 1) * P], ident_bf[:])
+                        nc.tensor.transpose(pt[:, Th, k, :], er3[i][:, 2 * j + Th, k * P:(k + 1) * P], ident_bf[:])
                 live[("pt", i, j)] = pt
             elif kind == "ee":
                 if ("eg", i) not in live:
@@ -175,7 +174,7 @@ def tile_yuyipointupdate_pa_kernel(tc, distribution_edge, instance_edge, point_n
                 b = i // 2
                 ec, es = live[("ec", i)]
                 cols = slice(j * P, (j + 1) * P)
-                ap = mm.tile([P, 4, P], F32, name="ap", tag="mm")
+                ap = psum.tile([P, 4, P], F32, name="ap", tag="ps")
                 for k in range(4):
                     fc = slice(k * P, (k + 1) * P)
                     nc.tensor.matmul_mx(
@@ -196,7 +195,7 @@ def tile_yuyipointupdate_pa_kernel(tc, distribution_edge, instance_edge, point_n
                 b = i // 2
                 nc.vector.quantize_mx(out=xc[b][:, i % 2, :].bitcast(FP8X4), scales=xs[b][:, i % 2, :], in_=live[("xg", i)][:].rearrange("p n k -> p (n k)"))
             elif kind == "wt":
-                wt = tp.tile([P, 2, 2, P], F32, name="wt", tag="tp")
+                wt = psum.tile([P, 2, 2, P], F32, name="wt", tag="ps")
                 for s in range(2):
                     w32 = wr[:, 2 * j + s, :].bitcast(F32)
                     for u in range(2):
@@ -213,17 +212,18 @@ def tile_yuyipointupdate_pa_kernel(tc, distribution_edge, instance_edge, point_n
             elif kind == "bn":
                 nc.vector.bn_stats(out=st[:, j, i, :], in_=live[("z", i, j)][:])
             elif kind == "ag":
-                for O in range(4 * i, 4 * i + 4):
+                lo, hi = GRP * i, GRP * (i + 1)
+                for O in range(lo, hi):
                     nc.vector.bn_aggr(out=mv[:, O, :], in_=st[:, O, :, :].rearrange("p b s -> p (b s)"))
+                nc.vector.tensor_tensor(out=gm[:, 1, lo:hi], in0=mv[:, lo:hi, 0], in1=gm[:, 0, lo:hi], op=ALU.mult)
             elif kind == "sq":
-                lo, hi = 4 * i, 4 * i + 4
+                lo, hi = GRP * i, GRP * (i + 1)
                 nc.scalar.activation(out=sd[:, lo:hi], in_=mv[:, lo:hi, 1], func=ACT.Sqrt, bias=eps_t[:, 0:1], scale=1.0)
             elif kind == "co":
-                lo, hi = 4 * i, 4 * i + 4
+                lo, hi = GRP * i, GRP * (i + 1)
                 nc.vector.reciprocal(out=rstd[:, lo:hi], in_=sd[:, lo:hi])
-                nc.vector.tensor_tensor(out=ca[:, lo:hi], in0=rstd[:, lo:hi], in1=gbT[:, lo:hi], op=ALU.mult)
-                nc.vector.tensor_tensor(out=cm[:, lo:hi], in0=mv[:, lo:hi, 0], in1=ca[:, lo:hi], op=ALU.mult)
-                nc.vector.tensor_tensor(out=cb[:, lo:hi], in0=gbT[:, NO + lo:NO + hi], in1=cm[:, lo:hi], op=ALU.subtract)
+                nc.vector.tensor_tensor(out=cc[:, :, lo:hi], in0=gm[:, :, lo:hi], in1=rstd[:, lo:hi].unsqueeze(1).to_broadcast([P, 2, GRP]), op=ALU.mult)
+                nc.vector.tensor_tensor(out=cb[:, lo:hi], in0=bT[:, lo:hi], in1=cc[:, 1, lo:hi], op=ALU.subtract)
             elif kind == "f":
                 live[("f", i, j)] = z_bank(i, j)
             elif kind == "af":
@@ -232,74 +232,75 @@ def tile_yuyipointupdate_pa_kernel(tc, distribution_edge, instance_edge, point_n
                 y = live[("y", i)]
                 z = live[("f", i, j)]
                 if engine == "V":
-                    nc.vector.tensor_scalar(out=y[:, j, :], in0=z[:], scalar1=ca[:, i:i + 1], scalar2=cb[:, i:i + 1], op0=ALU.mult, op1=ALU.add)
+                    nc.vector.tensor_scalar(out=y[:, j, :], in0=z[:], scalar1=cc[:, 0, i:i + 1], scalar2=cb[:, i:i + 1], op0=ALU.mult, op1=ALU.add)
                 else:
-                    nc.scalar.activation(out=y[:, j, :], in_=z[:], func=ACT.Identity, bias=cb[:, i:i + 1], scale=ca[:, i:i + 1])
+                    nc.scalar.activation(out=y[:, j, :], in_=z[:], func=ACT.Identity, bias=cb[:, i:i + 1], scale=cc[:, 0, i:i + 1])
             elif kind == "lr":
                 y = live[("y", i)]
-                yo = ypool.tile([P, B, N], F32, name="yo")
-                pieces = 2 if i == NO - 1 else 1
-                width = B // pieces
-                for q in range(pieces):
-                    bs = slice(q * width, (q + 1) * width)
-                    yf = y[:, bs, :].rearrange("p b n -> p (b n)")
-                    nc.vector.scalar_tensor_tensor(out=yo[:, bs, :].rearrange("p b n -> p (b n)"), in0=yf, scalar=NEG_SLOPE, in1=yf, op0=ALU.mult, op1=ALU.max)
-                    nc.sync.dma_start(out=out_view[i][:, bs, :], in_=yo[:, bs, :])
+                if ("yo", i) not in live:
+                    live[("yo", i)] = ypool.tile([P, B, N], F32, name="yo")
+                yo = live[("yo", i)]
+                width = B // (2 if i == NO - 1 else 1)
+                bs = slice(j * width, (j + 1) * width)
+                yf = y[:, bs, :].rearrange("p b n -> p (b n)")
+                nc.vector.scalar_tensor_tensor(out=yo[:, bs, :].rearrange("p b n -> p (b n)"), in0=yf, scalar=NEG_SLOPE, in1=yf, op0=ALU.mult, op1=ALU.max)
+                nc.sync.dma_start(out=out_view[i][:, bs, :], in_=yo[:, bs, :])
 
         for kind, i, j, engine in ORDER:
             step(kind, i, j, engine)
 
 
 ORDER = (
-    ("mk", 0, 0, "V"), ("ab", 0, 0, "S"), ("pr", 0, 0, "V"), ("qp", 0, 0, "V"), ("mk", 1, 0, "V"), ("sc", 0, 0, "V"),
-    ("ab", 1, 0, "S"), ("wt", 0, 0, "PE"), ("wt", 0, 1, "PE"), ("tr", 0, 0, "PE"), ("we", 0, 0, "S"), ("ee", 0, 0, "V"),
-    ("we", 0, 1, "S"), ("tr", 0, 1, "PE"), ("sc", 1, 0, "V"), ("wt", 0, 2, "PE"), ("wt", 0, 3, "PE"), ("ee", 0, 1, "V"),
-    ("we", 0, 2, "S"), ("we", 0, 3, "S"), ("qe", 0, 0, "V"), ("tr", 1, 0, "PE"), ("mk", 2, 0, "V"), ("tr", 1, 1, "PE"),
-    ("pr", 1, 0, "V"), ("ab", 2, 0, "S"), ("m", 0, 0, "PE"), ("m", 0, 1, "PE"), ("m", 0, 2, "PE"), ("ee", 1, 0, "V"),
-    ("m", 0, 3, "PE"), ("wt", 1, 0, "PE"), ("ee", 1, 1, "V"), ("wt", 1, 1, "PE"), ("ex", 0, 0, "S"), ("qe", 1, 0, "V"),
-    ("ex", 0, 1, "S"), ("wt", 1, 2, "PE"), ("qp", 1, 0, "V"), ("ex", 0, 2, "S"), ("m", 1, 0, "PE"), ("qw", 0, 0, "V"),
-    ("ex", 0, 3, "S"), ("m", 1, 1, "PE"), ("m", 1, 2, "PE"), ("we", 1, 0, "S"), ("m", 1, 3, "PE"), ("mk", 3, 0, "V"),
-    ("ex", 1, 0, "S"), ("qx", 0, 0, "V"), ("wt", 1, 3, "PE"), ("ex", 1, 1, "S"), ("sc", 2, 0, "V"), ("ex", 1, 2, "S"),
-    ("mk", 4, 0, "V"), ("ex", 1, 3, "S"), ("pr", 2, 0, "V"), ("we", 1, 1, "S"), ("we", 1, 2, "S"), ("qx", 1, 0, "V"),
-    ("tr", 2, 0, "PE"), ("we", 1, 3, "S"), ("qp", 2, 0, "V"), ("tr", 2, 1, "PE"), ("ab", 3, 0, "S"), ("mk", 5, 0, "V"),
-    ("qw", 1, 0, "V"), ("ee", 2, 1, "V"), ("z", 0, 0, "PE"), ("ee", 2, 0, "S"), ("z", 0, 1, "PE"), ("mk", 6, 0, "V"),
-    ("sc", 3, 0, "V"), ("z", 0, 2, "PE"), ("ab", 4, 0, "S"), ("z", 0, 3, "PE"), ("qe", 2, 0, "V"), ("z", 0, 4, "PE"),
-    ("bn", 0, 0, "V"), ("tr", 3, 0, "PE"), ("bn", 0, 1, "V"), ("tr", 3, 1, "PE"), ("bn", 0, 2, "V"), ("m", 2, 0, "PE"),
-    ("ee", 3, 0, "S"), ("m", 2, 1, "PE"), ("bn", 0, 3, "V"), ("m", 2, 2, "PE"), ("ee", 3, 1, "V"), ("ex", 2, 0, "S"),
-    ("m", 2, 3, "PE"), ("ex", 2, 1, "S"), ("qe", 3, 0, "V"), ("z", 0, 5, "PE"), ("ex", 2, 2, "S"), ("sc", 4, 0, "V"),
-    ("z", 0, 6, "PE"), ("ex", 2, 3, "S"), ("m", 3, 0, "PE"), ("ab", 5, 0, "S"), ("bn", 0, 4, "V"), ("m", 3, 1, "PE"),
-    ("qx", 2, 0, "V"), ("tr", 4, 0, "PE"), ("bn", 0, 5, "V"), ("m", 3, 2, "PE"), ("tr", 4, 1, "PE"), ("bn", 0, 6, "V"),
-    ("m", 3, 3, "PE"), ("pr", 3, 0, "V"), ("ex", 3, 0, "S"), ("z", 0, 7, "PE"), ("ex", 3, 1, "S"), ("ex", 3, 2, "S"),
-    ("ee", 4, 1, "V"), ("ex", 3, 3, "S"), ("ee", 4, 0, "S"), ("bn", 0, 7, "V"), ("qx", 3, 0, "V"), ("ab", 6, 0, "S"),
-    ("sc", 5, 0, "V"), ("z", 1, 0, "PE"), ("qe", 4, 0, "V"), ("z", 1, 1, "PE"), ("bn", 1, 0, "V"), ("z", 1, 2, "PE"),
-    ("m", 4, 0, "PE"), ("bn", 1, 1, "V"), ("m", 4, 1, "PE"), ("bn", 1, 2, "V"), ("m", 4, 2, "PE"), ("ex", 4, 0, "S"),
-    ("tr", 5, 0, "PE"), ("qp", 3, 0, "V"), ("ex", 4, 1, "S"), ("m", 4, 3, "PE"), ("mk", 7, 0, "V"), ("z", 1, 3, "PE"),
-    ("ex", 4, 2, "S"), ("sc", 6, 0, "V"), ("tr", 5, 1, "PE"), ("ex", 4, 3, "S"), ("z", 1, 4, "PE"), ("bn", 1, 3, "V"),
-    ("ee", 5, 0, "S"), ("z", 1, 5, "PE"), ("qx", 4, 0, "V"), ("z", 1, 6, "PE"), ("bn", 1, 4, "V"), ("ee", 5, 1, "S"),
-    ("z", 1, 7, "PE"), ("bn", 1, 5, "V"), ("tr", 6, 0, "PE"), ("bn", 1, 6, "V"), ("ab", 7, 0, "S"), ("tr", 6, 1, "PE"),
-    ("qe", 5, 0, "V"), ("bn", 1, 7, "V"), ("m", 5, 0, "PE"), ("m", 5, 1, "PE"), ("m", 5, 2, "PE"), ("m", 5, 3, "PE"),
-    ("ex", 5, 0, "S"), ("sc", 7, 0, "V"), ("ex", 5, 1, "S"), ("ex", 5, 2, "S"), ("ex", 5, 3, "S"), ("tr", 7, 0, "PE"),
-    ("ee", 6, 0, "S"), ("qx", 5, 0, "V"), ("ee", 6, 1, "S"), ("z", 2, 0, "PE"), ("z", 2, 1, "PE"), ("ee", 7, 0, "S"),
-    ("bn", 2, 0, "V"), ("z", 2, 2, "PE"), ("qe", 6, 0, "V"), ("z", 2, 3, "PE"), ("tr", 7, 1, "PE"), ("bn", 2, 1, "V"),
-    ("m", 6, 0, "PE"), ("bn", 2, 2, "V"), ("m", 6, 1, "PE"), ("ee", 7, 1, "S"), ("m", 6, 2, "PE"), ("bn", 2, 3, "V"),
-    ("m", 6, 3, "PE"), ("ex", 6, 0, "S"), ("z", 2, 4, "PE"), ("qe", 7, 0, "V"), ("ex", 6, 1, "S"), ("z", 2, 5, "PE"),
-    ("bn", 2, 4, "V"), ("ex", 6, 2, "S"), ("m", 7, 0, "PE"), ("ex", 6, 3, "S"), ("bn", 2, 5, "V"), ("m", 7, 1, "PE"),
-    ("ex", 7, 0, "S"), ("m", 7, 2, "PE"), ("qx", 6, 0, "V"), ("m", 7, 3, "PE"), ("ex", 7, 1, "S"), ("z", 2, 6, "PE"),
-    ("ex", 7, 2, "S"), ("z", 2, 7, "PE"), ("bn", 2, 6, "V"), ("ex", 7, 3, "S"), ("bn", 2, 7, "V"), ("qx", 7, 0, "V"),
-    ("z", 3, 0, "PE"), ("z", 3, 1, "PE"), ("bn", 3, 0, "V"), ("z", 3, 2, "PE"), ("bn", 3, 1, "V"), ("z", 3, 3, "PE"),
-    ("z", 3, 4, "PE"), ("bn", 3, 2, "V"), ("z", 3, 5, "PE"), ("bn", 3, 3, "V"), ("z", 3, 6, "PE"), ("bn", 3, 4, "V"),
-    ("z", 3, 7, "PE"), ("bn", 3, 5, "V"), ("bn", 3, 6, "V"), ("bn", 3, 7, "V"), ("ag", 0, 0, "V"), ("ag", 1, 0, "V"),
-    ("sq", 0, 0, "S"), ("sq", 1, 0, "S"), ("co", 0, 0, "V"), ("co", 1, 0, "V"), ("f", 0, 0, "PE"), ("f", 0, 1, "PE"),
-    ("af", 0, 0, "S"), ("f", 0, 2, "PE"), ("f", 0, 3, "PE"), ("af", 0, 1, "S"), ("f", 1, 0, "PE"), ("af", 0, 2, "S"),
-    ("af", 0, 3, "V"), ("f", 1, 1, "PE"), ("af", 1, 0, "S"), ("f", 1, 2, "PE"), ("lr", 0, 0, "V"), ("f", 1, 3, "PE"),
-    ("af", 1, 1, "S"), ("f", 2, 0, "PE"), ("af", 1, 2, "S"), ("f", 2, 1, "PE"), ("af", 1, 3, "S"), ("f", 2, 2, "PE"),
-    ("af", 2, 0, "S"), ("f", 2, 3, "PE"), ("lr", 1, 0, "V"), ("af", 2, 1, "S"), ("f", 3, 0, "PE"), ("f", 3, 1, "PE"),
-    ("af", 2, 2, "S"), ("f", 3, 2, "PE"), ("af", 2, 3, "S"), ("f", 3, 3, "PE"), ("af", 3, 0, "S"), ("lr", 2, 0, "V"),
-    ("f", 4, 0, "PE"), ("af", 3, 1, "S"), ("f", 4, 1, "PE"), ("af", 3, 2, "S"), ("f", 4, 2, "PE"), ("af", 4, 0, "S"),
-    ("f", 4, 3, "PE"), ("af", 4, 1, "S"), ("af", 3, 3, "V"), ("f", 5, 0, "PE"), ("af", 4, 2, "S"), ("lr", 3, 0, "V"),
-    ("f", 5, 1, "PE"), ("af", 4, 3, "S"), ("f", 5, 2, "PE"), ("af", 5, 0, "S"), ("f", 5, 3, "PE"), ("af", 5, 1, "S"),
-    ("f", 6, 0, "PE"), ("lr", 4, 0, "V"), ("af", 5, 2, "S"), ("f", 6, 1, "PE"), ("f", 6, 2, "PE"), ("af", 5, 3, "S"),
-    ("f", 6, 3, "PE"), ("af", 6, 0, "S"), ("lr", 5, 0, "V"), ("f", 7, 0, "PE"), ("af", 6, 1, "S"), ("f", 7, 1, "PE"),
-    ("af", 6, 2, "S"), ("f", 7, 2, "PE"), ("af", 7, 0, "S"), ("f", 7, 3, "PE"), ("af", 7, 1, "S"), ("af", 6, 3, "V"),
-    ("af", 7, 2, "S"), ("lr", 6, 0, "V"), ("af", 7, 3, "S"), ("lr", 7, 0, "V"),
+    ("mk", 0, 0, "V"), ("ab", 0, 0, "S"), ("pr", 0, 0, "V"), ("mk", 1, 0, "V"), ("qp", 0, 0, "V"), ("mk", 2, 0, "V"),
+    ("ab", 1, 0, "S"), ("sc", 0, 0, "V"), ("wt", 0, 0, "PE"), ("ab", 2, 0, "S"), ("tr", 0, 0, "PE"), ("sc", 1, 0, "V"),
+    ("tr", 0, 1, "PE"), ("wt", 0, 1, "PE"), ("ee", 0, 0, "V"), ("wt", 1, 0, "PE"), ("wt", 1, 1, "PE"), ("we", 0, 0, "S"),
+    ("tr", 1, 0, "PE"), ("ee", 0, 1, "V"), ("we", 0, 1, "S"), ("tr", 1, 1, "PE"), ("we", 1, 0, "S"), ("mk", 3, 0, "V"),
+    ("qe", 0, 0, "V"), ("wt", 0, 2, "PE"), ("we", 1, 1, "S"), ("sc", 2, 0, "V"), ("wt", 0, 3, "PE"), ("ab", 3, 0, "S"),
+    ("wt", 1, 2, "PE"), ("ee", 1, 0, "V"), ("m", 0, 0, "PE"), ("m", 0, 1, "PE"), ("m", 0, 2, "PE"), ("ee", 1, 1, "V"),
+    ("we", 0, 2, "S"), ("m", 0, 3, "PE"), ("pr", 1, 0, "V"), ("we", 0, 3, "S"), ("ex", 0, 0, "S"), ("wt", 1, 3, "PE"),
+    ("ex", 0, 1, "S"), ("tr", 2, 0, "PE"), ("qw", 0, 0, "V"), ("tr", 2, 1, "PE"), ("ex", 0, 2, "S"), ("ex", 0, 3, "S"),
+    ("qe", 1, 0, "V"), ("qp", 1, 0, "V"), ("we", 1, 2, "S"), ("mk", 4, 0, "V"), ("we", 1, 3, "S"), ("m", 1, 0, "PE"),
+    ("qx", 0, 0, "V"), ("m", 1, 1, "PE"), ("ee", 2, 0, "S"), ("m", 1, 2, "PE"), ("sc", 3, 0, "V"), ("m", 1, 3, "PE"),
+    ("ex", 1, 0, "S"), ("qw", 1, 0, "V"), ("ex", 1, 1, "S"), ("tr", 3, 0, "PE"), ("ex", 1, 2, "S"), ("ee", 2, 1, "V"),
+    ("tr", 3, 1, "PE"), ("ex", 1, 3, "S"), ("ab", 4, 0, "S"), ("mk", 5, 0, "V"), ("qe", 2, 0, "V"), ("qx", 1, 0, "V"),
+    ("ee", 3, 1, "V"), ("m", 2, 0, "PE"), ("m", 2, 1, "PE"), ("m", 2, 2, "PE"), ("ee", 3, 0, "S"), ("pr", 2, 0, "V"),
+    ("m", 2, 3, "PE"), ("z", 0, 0, "PE"), ("z", 0, 1, "PE"), ("ex", 2, 0, "S"), ("sc", 4, 0, "V"), ("z", 0, 2, "PE"),
+    ("ex", 2, 1, "S"), ("z", 0, 3, "PE"), ("ex", 2, 2, "S"), ("qe", 3, 0, "V"), ("z", 0, 4, "PE"), ("ex", 2, 3, "S"),
+    ("qp", 2, 0, "V"), ("tr", 4, 0, "PE"), ("ab", 5, 0, "S"), ("mk", 6, 0, "V"), ("bn", 0, 0, "V"), ("m", 3, 0, "PE"),
+    ("m", 3, 1, "PE"), ("qx", 2, 0, "V"), ("bn", 0, 1, "V"), ("m", 3, 2, "PE"), ("bn", 0, 2, "V"), ("ex", 3, 0, "S"),
+    ("bn", 0, 3, "V"), ("m", 3, 3, "PE"), ("ex", 3, 1, "S"), ("sc", 5, 0, "V"), ("tr", 4, 1, "PE"), ("ex", 3, 2, "S"),
+    ("z", 0, 5, "PE"), ("mk", 7, 0, "V"), ("ex", 3, 3, "S"), ("bn", 0, 4, "V"), ("z", 0, 6, "PE"), ("ee", 4, 0, "S"),
+    ("ee", 4, 1, "V"), ("z", 0, 7, "PE"), ("tr", 5, 0, "PE"), ("ab", 6, 0, "S"), ("qx", 3, 0, "V"), ("tr", 5, 1, "PE"),
+    ("qe", 4, 0, "V"), ("bn", 0, 5, "V"), ("z", 1, 0, "PE"), ("bn", 0, 6, "V"), ("m", 4, 0, "PE"), ("m", 4, 1, "PE"),
+    ("bn", 0, 7, "V"), ("ee", 5, 0, "S"), ("m", 4, 2, "PE"), ("ee", 5, 1, "V"), ("m", 4, 3, "PE"), ("ex", 4, 0, "S"),
+    ("z", 1, 1, "PE"), ("sc", 6, 0, "V"), ("ex", 4, 1, "S"), ("z", 1, 2, "PE"), ("ex", 4, 2, "S"), ("z", 1, 3, "PE"),
+    ("qe", 5, 0, "V"), ("ex", 4, 3, "S"), ("z", 1, 4, "PE"), ("pr", 3, 0, "V"), ("ab", 7, 0, "S"), ("tr", 6, 0, "PE"),
+    ("m", 5, 0, "PE"), ("m", 5, 1, "PE"), ("qx", 4, 0, "V"), ("qp", 3, 0, "V"), ("bn", 1, 0, "V"), ("ex", 5, 0, "S"),
+    ("bn", 1, 1, "V"), ("ex", 5, 1, "S"), ("sc", 7, 0, "V"), ("m", 5, 2, "PE"), ("ee", 6, 0, "S"), ("m", 5, 3, "PE"),
+    ("tr", 6, 1, "PE"), ("bn", 1, 2, "V"), ("ex", 5, 2, "S"), ("z", 1, 5, "PE"), ("bn", 1, 3, "V"), ("ex", 5, 3, "S"),
+    ("z", 1, 6, "PE"), ("bn", 1, 4, "V"), ("ee", 6, 1, "S"), ("z", 1, 7, "PE"), ("bn", 1, 5, "V"), ("qx", 5, 0, "V"),
+    ("tr", 7, 0, "PE"), ("tr", 7, 1, "PE"), ("bn", 1, 6, "V"), ("qe", 6, 0, "V"), ("ee", 7, 0, "S"), ("z", 2, 0, "PE"),
+    ("bn", 1, 7, "V"), ("z", 2, 1, "PE"), ("ee", 7, 1, "S"), ("m", 6, 0, "PE"), ("bn", 2, 0, "V"), ("m", 6, 1, "PE"),
+    ("m", 6, 2, "PE"), ("bn", 2, 1, "V"), ("m", 6, 3, "PE"), ("ex", 6, 0, "S"), ("z", 2, 2, "PE"), ("ex", 6, 1, "S"),
+    ("qe", 7, 0, "V"), ("z", 2, 3, "PE"), ("ex", 6, 2, "S"), ("z", 2, 4, "PE"), ("bn", 2, 2, "V"), ("ex", 6, 3, "S"),
+    ("z", 2, 5, "PE"), ("bn", 2, 3, "V"), ("m", 7, 0, "PE"), ("bn", 2, 4, "V"), ("m", 7, 1, "PE"), ("m", 7, 2, "PE"),
+    ("qx", 6, 0, "V"), ("m", 7, 3, "PE"), ("ex", 7, 0, "S"), ("z", 2, 6, "PE"), ("bn", 2, 5, "V"), ("ex", 7, 1, "S"),
+    ("z", 2, 7, "PE"), ("ex", 7, 2, "S"), ("bn", 2, 6, "V"), ("ex", 7, 3, "S"), ("bn", 2, 7, "V"), ("qx", 7, 0, "V"),
+    ("z", 3, 0, "PE"), ("z", 3, 1, "PE"), ("z", 3, 2, "PE"), ("bn", 3, 0, "V"), ("z", 3, 3, "PE"), ("bn", 3, 1, "V"),
+    ("z", 3, 4, "PE"), ("bn", 3, 2, "V"), ("z", 3, 5, "PE"), ("ag", 0, 0, "V"), ("bn", 3, 3, "V"), ("z", 3, 6, "PE"),
+    ("z", 3, 7, "PE"), ("bn", 3, 4, "V"), ("sq", 0, 0, "S"), ("f", 0, 0, "PE"), ("ag", 1, 0, "V"), ("bn", 3, 5, "V"),
+    ("f", 0, 1, "PE"), ("co", 0, 0, "V"), ("sq", 1, 0, "S"), ("f", 0, 2, "PE"), ("f", 0, 3, "PE"), ("ag", 2, 0, "V"),
+    ("bn", 3, 6, "V"), ("f", 1, 0, "PE"), ("af", 0, 0, "S"), ("co", 1, 0, "V"), ("f", 1, 1, "PE"), ("sq", 2, 0, "S"),
+    ("bn", 3, 7, "V"), ("f", 1, 2, "PE"), ("af", 0, 1, "S"), ("f", 1, 3, "PE"), ("af", 0, 3, "V"), ("af", 0, 2, "S"),
+    ("co", 2, 0, "V"), ("f", 2, 0, "PE"), ("af", 1, 0, "S"), ("f", 2, 1, "PE"), ("ag", 3, 0, "V"), ("af", 1, 1, "S"),
+    ("lr", 0, 0, "V"), ("f", 2, 2, "PE"), ("af", 1, 2, "S"), ("f", 2, 3, "PE"), ("sq", 3, 0, "S"), ("f", 3, 0, "PE"),
+    ("af", 1, 3, "S"), ("f", 3, 1, "PE"), ("af", 2, 0, "S"), ("co", 3, 0, "V"), ("f", 3, 2, "PE"), ("af", 2, 1, "S"),
+    ("f", 3, 3, "PE"), ("lr", 1, 0, "V"), ("af", 2, 2, "S"), ("f", 4, 0, "PE"), ("af", 2, 3, "S"), ("f", 4, 1, "PE"),
+    ("af", 3, 0, "S"), ("f", 4, 2, "PE"), ("af", 3, 3, "V"), ("af", 3, 1, "S"), ("f", 4, 3, "PE"), ("lr", 2, 0, "V"),
+    ("af", 3, 2, "S"), ("f", 5, 0, "PE"), ("f", 5, 1, "PE"), ("af", 4, 0, "S"), ("f", 5, 2, "PE"), ("af", 4, 1, "S"),
+    ("f", 5, 3, "PE"), ("lr", 3, 0, "V"), ("af", 4, 2, "S"), ("f", 6, 0, "PE"), ("af", 4, 3, "S"), ("f", 6, 1, "PE"),
+    ("af", 5, 0, "S"), ("f", 6, 2, "PE"), ("af", 5, 1, "S"), ("f", 6, 3, "PE"), ("lr", 4, 0, "V"), ("af", 5, 2, "S"),
+    ("f", 7, 0, "PE"), ("af", 5, 3, "S"), ("f", 7, 1, "PE"), ("af", 6, 0, "S"), ("f", 7, 2, "PE"), ("af", 6, 3, "V"),
+    ("af", 6, 1, "S"), ("f", 7, 3, "PE"), ("lr", 5, 0, "V"), ("af", 6, 2, "S"), ("af", 7, 0, "S"), ("af", 7, 1, "S"),
+    ("lr", 6, 0, "V"), ("af", 7, 2, "S"), ("af", 7, 3, "S"), ("lr", 7, 0, "V"), ("lr", 7, 1, "V"),
 )

@@ -209,6 +209,7 @@ def tile_yuyipointupdate_pa_kernel(tc, distribution_edge, instance_edge, point_n
                 nc.vector.quantize_mx(out=wc[:, i, :].bitcast(FP8X4), scales=ws[:, i, :], in_=wg[:, i * 4 * C:(i + 1) * 4 * C])
             elif kind == "z":
                 live[("z", i, j)] = z_bank(j, i)
+                live[("f", j, i)] = live[("z", i, j)]
             elif kind == "bn":
                 nc.vector.bn_stats(out=st[:, j, i, :], in_=live[("z", i, j)][:])
             elif kind == "ag":
@@ -227,80 +228,90 @@ def tile_yuyipointupdate_pa_kernel(tc, distribution_edge, instance_edge, point_n
             elif kind == "f":
                 live[("f", i, j)] = z_bank(i, j)
             elif kind == "af":
-                if ("y", i) not in live:
-                    live[("y", i)] = ypool.tile([P, B, N], F32, name="y")
-                y = live[("y", i)]
+                grp, pos = place[(i, j)]
+                if ("y", grp) not in live:
+                    live[("y", grp)] = ypool.tile([P, 4, N], F32, name="y")
+                y = live[("y", grp)]
                 z = live[("f", i, j)]
                 if engine == "V":
-                    nc.vector.tensor_scalar(out=y[:, j, :], in0=z[:], scalar1=cc[:, 0, i:i + 1], scalar2=cb[:, i:i + 1], op0=ALU.mult, op1=ALU.add)
+                    nc.vector.tensor_scalar(out=y[:, pos, :], in0=z[:], scalar1=cc[:, 0, i:i + 1], scalar2=cb[:, i:i + 1], op0=ALU.mult, op1=ALU.add)
                 else:
-                    nc.scalar.activation(out=y[:, j, :], in_=z[:], func=ACT.Identity, bias=cb[:, i:i + 1], scale=cc[:, 0, i:i + 1])
+                    nc.scalar.activation(out=y[:, pos, :], in_=z[:], func=ACT.Identity, bias=cb[:, i:i + 1], scale=cc[:, 0, i:i + 1])
             elif kind == "lr":
+                members = groups[i]
+                n = len(members)
                 y = live[("y", i)]
-                if ("yo", i) not in live:
-                    live[("yo", i)] = ypool.tile([P, B, N], F32, name="yo")
-                yo = live[("yo", i)]
-                width = B // (2 if i == NO - 1 else 1)
-                bs = slice(j * width, (j + 1) * width)
-                yf = y[:, bs, :].rearrange("p b n -> p (b n)")
-                nc.vector.scalar_tensor_tensor(out=yo[:, bs, :].rearrange("p b n -> p (b n)"), in0=yf, scalar=NEG_SLOPE, in1=yf, op0=ALU.mult, op1=ALU.max)
-                nc.sync.dma_start(out=out_view[i][:, bs, :], in_=yo[:, bs, :])
+                yo = ypool.tile([P, 4, N], F32, name="yo")
+                yf = y[:, 0:n, :].rearrange("p b n -> p (b n)")
+                nc.vector.scalar_tensor_tensor(out=yo[:, 0:n, :].rearrange("p b n -> p (b n)"), in0=yf, scalar=NEG_SLOPE, in1=yf, op0=ALU.mult, op1=ALU.max)
+                for pos, (O, b) in enumerate(members):
+                    nc.sync.dma_start(out=out[b, O * P:(O + 1) * P, :], in_=yo[:, pos, :])
+
+        groups = []
+        place = {}
+        at = 0
+        for size in GROUP_SIZES:
+            groups.append(FINAL[at:at + size])
+            for pos in range(size):
+                place[FINAL[at + pos]] = (len(groups) - 1, pos)
+            at += size
 
         for kind, i, j, engine in ORDER:
             step(kind, i, j, engine)
 
 
 ORDER = (
-    ("mk", 0, 0, "V"), ("ab", 0, 0, "S"), ("pr", 0, 0, "V"), ("mk", 1, 0, "V"), ("qp", 0, 0, "V"), ("mk", 2, 0, "V"),
-    ("ab", 1, 0, "S"), ("sc", 0, 0, "V"), ("wt", 0, 0, "PE"), ("ab", 2, 0, "S"), ("tr", 0, 0, "PE"), ("sc", 1, 0, "V"),
-    ("tr", 0, 1, "PE"), ("wt", 0, 1, "PE"), ("ee", 0, 0, "V"), ("wt", 1, 0, "PE"), ("wt", 1, 1, "PE"), ("we", 0, 0, "S"),
-    ("tr", 1, 0, "PE"), ("ee", 0, 1, "V"), ("we", 0, 1, "S"), ("tr", 1, 1, "PE"), ("we", 1, 0, "S"), ("mk", 3, 0, "V"),
-    ("qe", 0, 0, "V"), ("wt", 0, 2, "PE"), ("we", 1, 1, "S"), ("sc", 2, 0, "V"), ("wt", 0, 3, "PE"), ("ab", 3, 0, "S"),
-    ("wt", 1, 2, "PE"), ("ee", 1, 0, "V"), ("m", 0, 0, "PE"), ("m", 0, 1, "PE"), ("m", 0, 2, "PE"), ("ee", 1, 1, "V"),
-    ("we", 0, 2, "S"), ("m", 0, 3, "PE"), ("pr", 1, 0, "V"), ("we", 0, 3, "S"), ("ex", 0, 0, "S"), ("wt", 1, 3, "PE"),
-    ("ex", 0, 1, "S"), ("tr", 2, 0, "PE"), ("qw", 0, 0, "V"), ("tr", 2, 1, "PE"), ("ex", 0, 2, "S"), ("ex", 0, 3, "S"),
-    ("qe", 1, 0, "V"), ("qp", 1, 0, "V"), ("we", 1, 2, "S"), ("mk", 4, 0, "V"), ("we", 1, 3, "S"), ("m", 1, 0, "PE"),
-    ("qx", 0, 0, "V"), ("m", 1, 1, "PE"), ("ee", 2, 0, "S"), ("m", 1, 2, "PE"), ("sc", 3, 0, "V"), ("m", 1, 3, "PE"),
-    ("ex", 1, 0, "S"), ("qw", 1, 0, "V"), ("ex", 1, 1, "S"), ("tr", 3, 0, "PE"), ("ex", 1, 2, "S"), ("ee", 2, 1, "V"),
-    ("tr", 3, 1, "PE"), ("ex", 1, 3, "S"), ("ab", 4, 0, "S"), ("mk", 5, 0, "V"), ("qe", 2, 0, "V"), ("qx", 1, 0, "V"),
-    ("ee", 3, 1, "V"), ("m", 2, 0, "PE"), ("m", 2, 1, "PE"), ("m", 2, 2, "PE"), ("ee", 3, 0, "S"), ("pr", 2, 0, "V"),
-    ("m", 2, 3, "PE"), ("z", 0, 0, "PE"), ("z", 0, 1, "PE"), ("ex", 2, 0, "S"), ("sc", 4, 0, "V"), ("z", 0, 2, "PE"),
-    ("ex", 2, 1, "S"), ("z", 0, 3, "PE"), ("ex", 2, 2, "S"), ("qe", 3, 0, "V"), ("z", 0, 4, "PE"), ("ex", 2, 3, "S"),
-    ("qp", 2, 0, "V"), ("tr", 4, 0, "PE"), ("ab", 5, 0, "S"), ("mk", 6, 0, "V"), ("bn", 0, 0, "V"), ("m", 3, 0, "PE"),
-    ("m", 3, 1, "PE"), ("qx", 2, 0, "V"), ("bn", 0, 1, "V"), ("m", 3, 2, "PE"), ("bn", 0, 2, "V"), ("ex", 3, 0, "S"),
-    ("bn", 0, 3, "V"), ("m", 3, 3, "PE"), ("ex", 3, 1, "S"), ("sc", 5, 0, "V"), ("tr", 4, 1, "PE"), ("ex", 3, 2, "S"),
-    ("z", 0, 5, "PE"), ("mk", 7, 0, "V"), ("ex", 3, 3, "S"), ("bn", 0, 4, "V"), ("z", 0, 6, "PE"), ("ee", 4, 0, "S"),
-    ("ee", 4, 1, "V"), ("z", 0, 7, "PE"), ("tr", 5, 0, "PE"), ("ab", 6, 0, "S"), ("qx", 3, 0, "V"), ("tr", 5, 1, "PE"),
-    ("qe", 4, 0, "V"), ("bn", 0, 5, "V"), ("z", 1, 0, "PE"), ("bn", 0, 6, "V"), ("m", 4, 0, "PE"), ("m", 4, 1, "PE"),
-    ("bn", 0, 7, "V"), ("ee", 5, 0, "S"), ("m", 4, 2, "PE"), ("ee", 5, 1, "V"), ("m", 4, 3, "PE"), ("ex", 4, 0, "S"),
-    ("z", 1, 1, "PE"), ("sc", 6, 0, "V"), ("ex", 4, 1, "S"), ("z", 1, 2, "PE"), ("ex", 4, 2, "S"), ("z", 1, 3, "PE"),
-    ("qe", 5, 0, "V"), ("ex", 4, 3, "S"), ("z", 1, 4, "PE"), ("pr", 3, 0, "V"), ("ab", 7, 0, "S"), ("tr", 6, 0, "PE"),
-    ("m", 5, 0, "PE"), ("m", 5, 1, "PE"), ("qx", 4, 0, "V"), ("qp", 3, 0, "V"), ("bn", 1, 0, "V"), ("ex", 5, 0, "S"),
-    ("bn", 1, 1, "V"), ("ex", 5, 1, "S"), ("sc", 7, 0, "V"), ("m", 5, 2, "PE"), ("ee", 6, 0, "S"), ("m", 5, 3, "PE"),
-    ("tr", 6, 1, "PE"), ("bn", 1, 2, "V"), ("ex", 5, 2, "S"), ("z", 1, 5, "PE"), ("bn", 1, 3, "V"), ("ex", 5, 3, "S"),
-    ("z", 1, 6, "PE"), ("bn", 1, 4, "V"), ("ee", 6, 1, "S"), ("z", 1, 7, "PE"), ("bn", 1, 5, "V"), ("qx", 5, 0, "V"),
-    ("tr", 7, 0, "PE"), ("tr", 7, 1, "PE"), ("bn", 1, 6, "V"), ("qe", 6, 0, "V"), ("ee", 7, 0, "S"), ("z", 2, 0, "PE"),
-    ("bn", 1, 7, "V"), ("z", 2, 1, "PE"), ("ee", 7, 1, "S"), ("m", 6, 0, "PE"), ("bn", 2, 0, "V"), ("m", 6, 1, "PE"),
-    ("m", 6, 2, "PE"), ("bn", 2, 1, "V"), ("m", 6, 3, "PE"), ("ex", 6, 0, "S"), ("z", 2, 2, "PE"), ("ex", 6, 1, "S"),
-    ("qe", 7, 0, "V"), ("z", 2, 3, "PE"), ("ex", 6, 2, "S"), ("z", 2, 4, "PE"), ("bn", 2, 2, "V"), ("ex", 6, 3, "S"),
-    ("z", 2, 5, "PE"), ("bn", 2, 3, "V"), ("m", 7, 0, "PE"), ("bn", 2, 4, "V"), ("m", 7, 1, "PE"), ("m", 7, 2, "PE"),
-    ("qx", 6, 0, "V"), ("m", 7, 3, "PE"), ("ex", 7, 0, "S"), ("z", 2, 6, "PE"), ("bn", 2, 5, "V"), ("ex", 7, 1, "S"),
-    ("z", 2, 7, "PE"), ("ex", 7, 2, "S"), ("bn", 2, 6, "V"), ("ex", 7, 3, "S"), ("bn", 2, 7, "V"), ("qx", 7, 0, "V"),
-    ("z", 3, 0, "PE"), ("z", 3, 1, "PE"), ("z", 3, 2, "PE"), ("bn", 3, 0, "V"), ("z", 3, 3, "PE"), ("bn", 3, 1, "V"),
-    ("z", 3, 4, "PE"), ("bn", 3, 2, "V"), ("z", 3, 5, "PE"), ("ag", 0, 0, "V"), ("bn", 3, 3, "V"), ("z", 3, 6, "PE"),
-    ("z", 3, 7, "PE"), ("bn", 3, 4, "V"), ("sq", 0, 0, "S"), ("f", 0, 0, "PE"), ("ag", 1, 0, "V"), ("bn", 3, 5, "V"),
-    ("f", 0, 1, "PE"), ("co", 0, 0, "V"), ("sq", 1, 0, "S"), ("f", 0, 2, "PE"), ("f", 0, 3, "PE"), ("ag", 2, 0, "V"),
-    ("bn", 3, 6, "V"), ("f", 1, 0, "PE"), ("af", 0, 0, "S"), ("co", 1, 0, "V"), ("f", 1, 1, "PE"), ("sq", 2, 0, "S"),
-    ("bn", 3, 7, "V"), ("f", 1, 2, "PE"), ("af", 0, 1, "S"), ("f", 1, 3, "PE"), ("af", 0, 3, "V"), ("af", 0, 2, "S"),
-    ("co", 2, 0, "V"), ("f", 2, 0, "PE"), ("af", 1, 0, "S"), ("f", 2, 1, "PE"), ("ag", 3, 0, "V"), ("af", 1, 1, "S"),
-    ("lr", 0, 0, "V"), ("f", 2, 2, "PE"), ("af", 1, 2, "S"), ("f", 2, 3, "PE"), ("sq", 3, 0, "S"), ("f", 3, 0, "PE"),
-    ("af", 1, 3, "S"), ("f", 3, 1, "PE"), ("af", 2, 0, "S"), ("co", 3, 0, "V"), ("f", 3, 2, "PE"), ("af", 2, 1, "S"),
-    ("f", 3, 3, "PE"), ("lr", 1, 0, "V"), ("af", 2, 2, "S"), ("f", 4, 0, "PE"), ("af", 2, 3, "S"), ("f", 4, 1, "PE"),
-    ("af", 3, 0, "S"), ("f", 4, 2, "PE"), ("af", 3, 3, "V"), ("af", 3, 1, "S"), ("f", 4, 3, "PE"), ("lr", 2, 0, "V"),
-    ("af", 3, 2, "S"), ("f", 5, 0, "PE"), ("f", 5, 1, "PE"), ("af", 4, 0, "S"), ("f", 5, 2, "PE"), ("af", 4, 1, "S"),
-    ("f", 5, 3, "PE"), ("lr", 3, 0, "V"), ("af", 4, 2, "S"), ("f", 6, 0, "PE"), ("af", 4, 3, "S"), ("f", 6, 1, "PE"),
-    ("af", 5, 0, "S"), ("f", 6, 2, "PE"), ("af", 5, 1, "S"), ("f", 6, 3, "PE"), ("lr", 4, 0, "V"), ("af", 5, 2, "S"),
-    ("f", 7, 0, "PE"), ("af", 5, 3, "S"), ("f", 7, 1, "PE"), ("af", 6, 0, "S"), ("f", 7, 2, "PE"), ("af", 6, 3, "V"),
-    ("af", 6, 1, "S"), ("f", 7, 3, "PE"), ("lr", 5, 0, "V"), ("af", 6, 2, "S"), ("af", 7, 0, "S"), ("af", 7, 1, "S"),
-    ("lr", 6, 0, "V"), ("af", 7, 2, "S"), ("af", 7, 3, "S"), ("lr", 7, 0, "V"), ("lr", 7, 1, "V"),
+    ("mk", 0, 0, "V"), ("pr", 0, 0, "V"), ("ab", 0, 0, "S"), ("mk", 1, 0, "V"), ("qp", 0, 0, "V"), ("mk", 2, 0, "V"),
+    ("ab", 1, 0, "S"), ("sc", 0, 0, "V"), ("wt", 0, 0, "PE"), ("wt", 0, 1, "PE"), ("ab", 2, 0, "S"), ("tr", 0, 0, "PE"),
+    ("mk", 3, 0, "V"), ("tr", 0, 1, "PE"), ("sc", 1, 0, "V"), ("wt", 1, 0, "PE"), ("ee", 0, 0, "V"), ("wt", 1, 1, "PE"),
+    ("we", 0, 0, "S"), ("tr", 1, 0, "PE"), ("ee", 0, 1, "V"), ("we", 0, 1, "S"), ("tr", 1, 1, "PE"), ("ab", 3, 0, "S"),
+    ("wt", 0, 2, "PE"), ("sc", 2, 0, "V"), ("wt", 0, 3, "PE"), ("wt", 1, 2, "PE"), ("qe", 0, 0, "V"), ("wt", 1, 3, "PE"),
+    ("mk", 4, 0, "V"), ("ee", 1, 0, "V"), ("we", 0, 2, "S"), ("we", 0, 3, "S"), ("ee", 1, 1, "V"), ("we", 1, 0, "S"),
+    ("m", 0, 0, "PE"), ("we", 1, 1, "S"), ("sc", 3, 0, "V"), ("m", 0, 1, "PE"), ("m", 0, 2, "PE"), ("we", 1, 2, "S"),
+    ("m", 0, 3, "PE"), ("qw", 0, 0, "V"), ("we", 1, 3, "S"), ("tr", 2, 0, "PE"), ("ex", 0, 0, "S"), ("tr", 2, 1, "PE"),
+    ("qe", 1, 0, "V"), ("ex", 0, 1, "S"), ("tr", 3, 0, "PE"), ("pr", 1, 0, "V"), ("ex", 0, 2, "S"), ("tr", 3, 1, "PE"),
+    ("ex", 0, 3, "S"), ("m", 1, 0, "PE"), ("ab", 4, 0, "S"), ("qw", 1, 0, "V"), ("m", 1, 1, "PE"), ("m", 1, 2, "PE"),
+    ("m", 1, 3, "PE"), ("qx", 0, 0, "V"), ("qp", 1, 0, "V"), ("mk", 5, 0, "V"), ("ex", 1, 0, "S"), ("ee", 2, 1, "V"),
+    ("ex", 1, 1, "S"), ("ex", 1, 2, "S"), ("sc", 4, 0, "V"), ("ex", 1, 3, "S"), ("mk", 6, 0, "V"), ("ee", 2, 0, "S"),
+    ("ee", 3, 1, "V"), ("tr", 4, 0, "PE"), ("ab", 5, 0, "S"), ("qx", 1, 0, "V"), ("tr", 4, 1, "PE"), ("pr", 2, 0, "V"),
+    ("z", 0, 0, "PE"), ("qe", 2, 0, "V"), ("z", 0, 1, "PE"), ("ee", 3, 0, "S"), ("qp", 2, 0, "V"), ("z", 0, 2, "PE"),
+    ("mk", 7, 0, "V"), ("z", 0, 3, "PE"), ("sc", 5, 0, "V"), ("ab", 6, 0, "S"), ("m", 2, 0, "PE"), ("bn", 0, 0, "V"),
+    ("m", 2, 1, "PE"), ("bn", 0, 1, "V"), ("bn", 0, 2, "V"), ("m", 2, 2, "PE"), ("ex", 2, 0, "S"), ("bn", 0, 3, "V"),
+    ("m", 2, 3, "PE"), ("ex", 2, 1, "S"), ("qe", 3, 0, "V"), ("z", 0, 4, "PE"), ("sc", 6, 0, "V"), ("ex", 2, 2, "S"),
+    ("z", 0, 5, "PE"), ("ex", 2, 3, "S"), ("z", 0, 6, "PE"), ("ee", 4, 1, "V"), ("ee", 4, 0, "S"), ("m", 3, 0, "PE"),
+    ("m", 3, 1, "PE"), ("bn", 0, 4, "V"), ("m", 3, 2, "PE"), ("ab", 7, 0, "S"), ("qx", 2, 0, "V"), ("m", 3, 3, "PE"),
+    ("bn", 0, 5, "V"), ("z", 0, 7, "PE"), ("bn", 0, 6, "V"), ("tr", 5, 0, "PE"), ("qe", 4, 0, "V"), ("tr", 5, 1, "PE"),
+    ("ex", 3, 0, "S"), ("bn", 0, 7, "V"), ("tr", 6, 0, "PE"), ("ex", 3, 1, "S"), ("pr", 3, 0, "V"), ("ex", 3, 2, "S"),
+    ("m", 4, 0, "PE"), ("ex", 3, 3, "S"), ("m", 4, 1, "PE"), ("sc", 7, 0, "V"), ("m", 4, 2, "PE"), ("ee", 5, 0, "S"),
+    ("m", 4, 3, "PE"), ("ee", 5, 1, "V"), ("tr", 6, 1, "PE"), ("ex", 4, 0, "S"), ("ex", 4, 1, "S"), ("qx", 3, 0, "V"),
+    ("tr", 7, 0, "PE"), ("ex", 4, 2, "S"), ("qe", 5, 0, "V"), ("tr", 7, 1, "PE"), ("ex", 4, 3, "S"), ("qp", 3, 0, "V"),
+    ("z", 1, 0, "PE"), ("ee", 6, 0, "S"), ("z", 1, 1, "PE"), ("qx", 4, 0, "V"), ("z", 1, 2, "PE"), ("ee", 6, 1, "S"),
+    ("bn", 1, 0, "V"), ("z", 1, 3, "PE"), ("m", 5, 0, "PE"), ("bn", 1, 1, "V"), ("ee", 7, 0, "S"), ("bn", 1, 2, "V"),
+    ("m", 5, 1, "PE"), ("bn", 1, 3, "V"), ("ee", 7, 1, "S"), ("m", 5, 2, "PE"), ("m", 5, 3, "PE"), ("qe", 6, 0, "V"),
+    ("z", 1, 4, "PE"), ("ex", 5, 0, "S"), ("z", 1, 5, "PE"), ("ex", 5, 1, "S"), ("z", 1, 6, "PE"), ("qe", 7, 0, "V"),
+    ("ex", 5, 2, "S"), ("z", 1, 7, "PE"), ("bn", 1, 4, "V"), ("ex", 5, 3, "S"), ("m", 6, 0, "PE"), ("bn", 1, 5, "V"),
+    ("m", 6, 1, "PE"), ("bn", 1, 6, "V"), ("m", 6, 2, "PE"), ("m", 6, 3, "PE"), ("ex", 6, 0, "S"), ("bn", 1, 7, "V"),
+    ("m", 7, 0, "PE"), ("m", 7, 1, "PE"), ("ex", 6, 1, "S"), ("qx", 5, 0, "V"), ("m", 7, 2, "PE"), ("ex", 6, 2, "S"),
+    ("m", 7, 3, "PE"), ("ex", 6, 3, "S"), ("z", 2, 0, "PE"), ("ex", 7, 0, "S"), ("z", 2, 1, "PE"), ("ex", 7, 1, "S"),
+    ("z", 2, 2, "PE"), ("qx", 6, 0, "V"), ("ex", 7, 2, "S"), ("z", 2, 3, "PE"), ("bn", 2, 0, "V"), ("ex", 7, 3, "S"),
+    ("z", 2, 4, "PE"), ("bn", 2, 1, "V"), ("z", 2, 5, "PE"), ("bn", 2, 2, "V"), ("z", 2, 6, "PE"), ("bn", 2, 3, "V"),
+    ("z", 2, 7, "PE"), ("qx", 7, 0, "V"), ("bn", 2, 4, "V"), ("bn", 2, 5, "V"), ("z", 3, 0, "PE"), ("bn", 2, 6, "V"),
+    ("z", 3, 1, "PE"), ("bn", 2, 7, "V"), ("z", 3, 2, "PE"), ("bn", 3, 0, "V"), ("z", 3, 3, "PE"), ("bn", 3, 1, "V"),
+    ("z", 3, 4, "PE"), ("bn", 3, 2, "V"), ("z", 3, 5, "PE"), ("z", 3, 6, "PE"), ("ag", 0, 0, "V"), ("bn", 3, 3, "V"),
+    ("z", 3, 7, "PE"), ("bn", 3, 4, "V"), ("sq", 0, 0, "S"), ("ag", 1, 0, "V"), ("bn", 3, 5, "V"), ("bn", 3, 6, "V"),
+    ("sq", 1, 0, "S"), ("co", 0, 0, "V"), ("ag", 2, 0, "V"), ("f", 0, 0, "PE"), ("bn", 3, 7, "V"), ("co", 1, 0, "V"),
+    ("af", 0, 3, "S"), ("ag", 3, 0, "V"), ("sq", 2, 0, "S"), ("f", 0, 1, "PE"), ("af", 1, 3, "S"), ("af", 0, 0, "S"),
+    ("f", 0, 2, "PE"), ("co", 2, 0, "V"), ("sq", 3, 0, "S"), ("af", 0, 1, "S"), ("f", 1, 0, "PE"), ("af", 5, 3, "V"),
+    ("af", 2, 3, "S"), ("f", 1, 1, "PE"), ("co", 3, 0, "V"), ("af", 3, 3, "S"), ("f", 1, 2, "PE"), ("lr", 0, 0, "V"),
+    ("af", 0, 2, "S"), ("f", 2, 0, "PE"), ("af", 1, 0, "S"), ("f", 2, 1, "PE"), ("f", 2, 2, "PE"), ("af", 4, 3, "S"),
+    ("f", 3, 0, "PE"), ("af", 1, 1, "S"), ("lr", 1, 0, "V"), ("f", 3, 1, "PE"), ("af", 1, 2, "S"), ("f", 3, 2, "PE"),
+    ("af", 2, 0, "S"), ("f", 4, 0, "PE"), ("af", 2, 1, "S"), ("f", 4, 1, "PE"), ("lr", 2, 0, "V"), ("af", 2, 2, "S"),
+    ("f", 4, 2, "PE"), ("af", 3, 0, "S"), ("f", 5, 0, "PE"), ("af", 3, 1, "S"), ("f", 5, 1, "PE"), ("af", 3, 2, "S"),
+    ("af", 4, 1, "V"), ("f", 5, 2, "PE"), ("af", 4, 0, "S"), ("lr", 3, 0, "V"), ("f", 6, 0, "PE"), ("af", 4, 2, "S"),
+    ("f", 6, 1, "PE"), ("af", 5, 0, "S"), ("f", 6, 2, "PE"), ("af", 5, 1, "S"), ("f", 6, 3, "PE"), ("lr", 4, 0, "V"),
+    ("f", 7, 0, "PE"), ("af", 5, 2, "S"), ("f", 7, 1, "PE"), ("af", 6, 0, "S"), ("f", 7, 2, "PE"), ("af", 6, 1, "S"),
+    ("f", 7, 3, "PE"), ("lr", 5, 0, "V"), ("af", 6, 2, "S"), ("af", 7, 0, "S"), ("af", 7, 1, "S"), ("af", 7, 2, "S"),
+    ("af", 6, 3, "V"), ("af", 7, 3, "S"), ("lr", 6, 0, "V"), ("lr", 7, 0, "V"), ("lr", 8, 0, "V"), ("lr", 9, 0, "V"),
 )
+FINAL = ((0, 3), (1, 3), (0, 0), (0, 1), (2, 3), (3, 3), (0, 2), (1, 0), (4, 3), (5, 3), (1, 1), (1, 2), (2, 0), (2, 1), (2, 2), (3, 0), (3, 1), (3, 2), (4, 0), (4, 1), (4, 2), (5, 0), (5, 1), (5, 2), (6, 0), (6, 1), (6, 2), (6, 3), (7, 0), (7, 1), (7, 2), (7, 3))
+GROUP_SIZES = (4, 4, 4, 4, 4, 4, 4, 2, 1, 1)

@@ -209,7 +209,6 @@ def tile_yuyipointupdate_pa_kernel(tc, distribution_edge, instance_edge, point_n
                 nc.vector.quantize_mx(out=wc[:, i, :].bitcast(FP8X4), scales=ws[:, i, :], in_=wg[:, i * 4 * C:(i + 1) * 4 * C])
             elif kind == "z":
                 live[("z", i, j)] = z_bank(j, i)
-                live[("f", j, i)] = live[("z", i, j)]
             elif kind == "bn":
                 nc.vector.bn_stats(out=st[:, j, i, :], in_=live[("z", i, j)][:])
             elif kind == "ag":
@@ -228,90 +227,80 @@ def tile_yuyipointupdate_pa_kernel(tc, distribution_edge, instance_edge, point_n
             elif kind == "f":
                 live[("f", i, j)] = z_bank(i, j)
             elif kind == "af":
-                grp, pos = place[(i, j)]
-                if ("y", grp) not in live:
-                    live[("y", grp)] = ypool.tile([P, 4, N], F32, name="y")
-                y = live[("y", grp)]
+                if ("y", i) not in live:
+                    live[("y", i)] = ypool.tile([P, B, N], F32, name="y")
+                y = live[("y", i)]
                 z = live[("f", i, j)]
                 if engine == "V":
-                    nc.vector.tensor_scalar(out=y[:, pos, :], in0=z[:], scalar1=cc[:, 0, i:i + 1], scalar2=cb[:, i:i + 1], op0=ALU.mult, op1=ALU.add)
+                    nc.vector.tensor_scalar(out=y[:, j, :], in0=z[:], scalar1=cc[:, 0, i:i + 1], scalar2=cb[:, i:i + 1], op0=ALU.mult, op1=ALU.add)
                 else:
-                    nc.scalar.activation(out=y[:, pos, :], in_=z[:], func=ACT.Identity, bias=cb[:, i:i + 1], scale=cc[:, 0, i:i + 1])
+                    nc.scalar.activation(out=y[:, j, :], in_=z[:], func=ACT.Identity, bias=cb[:, i:i + 1], scale=cc[:, 0, i:i + 1])
             elif kind == "lr":
-                members = groups[i]
-                n = len(members)
                 y = live[("y", i)]
-                yo = ypool.tile([P, 4, N], F32, name="yo")
-                yf = y[:, 0:n, :].rearrange("p b n -> p (b n)")
-                nc.vector.scalar_tensor_tensor(out=yo[:, 0:n, :].rearrange("p b n -> p (b n)"), in0=yf, scalar=NEG_SLOPE, in1=yf, op0=ALU.mult, op1=ALU.max)
-                for pos, (O, b) in enumerate(members):
-                    nc.sync.dma_start(out=out[b, O * P:(O + 1) * P, :], in_=yo[:, pos, :])
-
-        groups = []
-        place = {}
-        at = 0
-        for size in GROUP_SIZES:
-            groups.append(FINAL[at:at + size])
-            for pos in range(size):
-                place[FINAL[at + pos]] = (len(groups) - 1, pos)
-            at += size
+                if ("yo", i) not in live:
+                    live[("yo", i)] = ypool.tile([P, B, N], F32, name="yo")
+                yo = live[("yo", i)]
+                width = B // (2 if i == NO - 1 else 1)
+                bs = slice(j * width, (j + 1) * width)
+                yf = y[:, bs, :].rearrange("p b n -> p (b n)")
+                nc.vector.scalar_tensor_tensor(out=yo[:, bs, :].rearrange("p b n -> p (b n)"), in0=yf, scalar=NEG_SLOPE, in1=yf, op0=ALU.mult, op1=ALU.max)
+                nc.sync.dma_start(out=out_view[i][:, bs, :], in_=yo[:, bs, :])
 
         for kind, i, j, engine in ORDER:
             step(kind, i, j, engine)
 
 
 ORDER = (
-    ("mk", 0, 0, "V"), ("pr", 0, 0, "V"), ("ab", 0, 0, "S"), ("mk", 1, 0, "V"), ("qp", 0, 0, "V"), ("mk", 2, 0, "V"),
-    ("ab", 1, 0, "S"), ("sc", 0, 0, "V"), ("wt", 0, 0, "PE"), ("wt", 0, 1, "PE"), ("ab", 2, 0, "S"), ("tr", 0, 0, "PE"),
-    ("mk", 3, 0, "V"), ("tr", 0, 1, "PE"), ("sc", 1, 0, "V"), ("wt", 1, 0, "PE"), ("ee", 0, 0, "V"), ("wt", 1, 1, "PE"),
-    ("we", 0, 0, "S"), ("tr", 1, 0, "PE"), ("ee", 0, 1, "V"), ("we", 0, 1, "S"), ("tr", 1, 1, "PE"), ("ab", 3, 0, "S"),
-    ("wt", 0, 2, "PE"), ("sc", 2, 0, "V"), ("wt", 0, 3, "PE"), ("wt", 1, 2, "PE"), ("qe", 0, 0, "V"), ("wt", 1, 3, "PE"),
-    ("mk", 4, 0, "V"), ("ee", 1, 0, "V"), ("we", 0, 2, "S"), ("we", 0, 3, "S"), ("ee", 1, 1, "V"), ("we", 1, 0, "S"),
-    ("m", 0, 0, "PE"), ("we", 1, 1, "S"), ("sc", 3, 0, "V"), ("m", 0, 1, "PE"), ("m", 0, 2, "PE"), ("we", 1, 2, "S"),
-    ("m", 0, 3, "PE"), ("qw", 0, 0, "V"), ("we", 1, 3, "S"), ("tr", 2, 0, "PE"), ("ex", 0, 0, "S"), ("tr", 2, 1, "PE"),
-    ("qe", 1, 0, "V"), ("ex", 0, 1, "S"), ("tr", 3, 0, "PE"), ("pr", 1, 0, "V"), ("ex", 0, 2, "S"), ("tr", 3, 1, "PE"),
-    ("ex", 0, 3, "S"), ("m", 1, 0, "PE"), ("ab", 4, 0, "S"), ("qw", 1, 0, "V"), ("m", 1, 1, "PE"), ("m", 1, 2, "PE"),
-    ("m", 1, 3, "PE"), ("qx", 0, 0, "V"), ("qp", 1, 0, "V"), ("mk", 5, 0, "V"), ("ex", 1, 0, "S"), ("ee", 2, 1, "V"),
-    ("ex", 1, 1, "S"), ("ex", 1, 2, "S"), ("sc", 4, 0, "V"), ("ex", 1, 3, "S"), ("mk", 6, 0, "V"), ("ee", 2, 0, "S"),
-    ("ee", 3, 1, "V"), ("tr", 4, 0, "PE"), ("ab", 5, 0, "S"), ("qx", 1, 0, "V"), ("tr", 4, 1, "PE"), ("pr", 2, 0, "V"),
-    ("z", 0, 0, "PE"), ("qe", 2, 0, "V"), ("z", 0, 1, "PE"), ("ee", 3, 0, "S"), ("qp", 2, 0, "V"), ("z", 0, 2, "PE"),
-    ("mk", 7, 0, "V"), ("z", 0, 3, "PE"), ("sc", 5, 0, "V"), ("ab", 6, 0, "S"), ("m", 2, 0, "PE"), ("bn", 0, 0, "V"),
-    ("m", 2, 1, "PE"), ("bn", 0, 1, "V"), ("bn", 0, 2, "V"), ("m", 2, 2, "PE"), ("ex", 2, 0, "S"), ("bn", 0, 3, "V"),
-    ("m", 2, 3, "PE"), ("ex", 2, 1, "S"), ("qe", 3, 0, "V"), ("z", 0, 4, "PE"), ("sc", 6, 0, "V"), ("ex", 2, 2, "S"),
-    ("z", 0, 5, "PE"), ("ex", 2, 3, "S"), ("z", 0, 6, "PE"), ("ee", 4, 1, "V"), ("ee", 4, 0, "S"), ("m", 3, 0, "PE"),
-    ("m", 3, 1, "PE"), ("bn", 0, 4, "V"), ("m", 3, 2, "PE"), ("ab", 7, 0, "S"), ("qx", 2, 0, "V"), ("m", 3, 3, "PE"),
-    ("bn", 0, 5, "V"), ("z", 0, 7, "PE"), ("bn", 0, 6, "V"), ("tr", 5, 0, "PE"), ("qe", 4, 0, "V"), ("tr", 5, 1, "PE"),
-    ("ex", 3, 0, "S"), ("bn", 0, 7, "V"), ("tr", 6, 0, "PE"), ("ex", 3, 1, "S"), ("pr", 3, 0, "V"), ("ex", 3, 2, "S"),
-    ("m", 4, 0, "PE"), ("ex", 3, 3, "S"), ("m", 4, 1, "PE"), ("sc", 7, 0, "V"), ("m", 4, 2, "PE"), ("ee", 5, 0, "S"),
-    ("m", 4, 3, "PE"), ("ee", 5, 1, "V"), ("tr", 6, 1, "PE"), ("ex", 4, 0, "S"), ("ex", 4, 1, "S"), ("qx", 3, 0, "V"),
-    ("tr", 7, 0, "PE"), ("ex", 4, 2, "S"), ("qe", 5, 0, "V"), ("tr", 7, 1, "PE"), ("ex", 4, 3, "S"), ("qp", 3, 0, "V"),
-    ("z", 1, 0, "PE"), ("ee", 6, 0, "S"), ("z", 1, 1, "PE"), ("qx", 4, 0, "V"), ("z", 1, 2, "PE"), ("ee", 6, 1, "S"),
-    ("bn", 1, 0, "V"), ("z", 1, 3, "PE"), ("m", 5, 0, "PE"), ("bn", 1, 1, "V"), ("ee", 7, 0, "S"), ("bn", 1, 2, "V"),
-    ("m", 5, 1, "PE"), ("bn", 1, 3, "V"), ("ee", 7, 1, "S"), ("m", 5, 2, "PE"), ("m", 5, 3, "PE"), ("qe", 6, 0, "V"),
-    ("z", 1, 4, "PE"), ("ex", 5, 0, "S"), ("z", 1, 5, "PE"), ("ex", 5, 1, "S"), ("z", 1, 6, "PE"), ("qe", 7, 0, "V"),
-    ("ex", 5, 2, "S"), ("z", 1, 7, "PE"), ("bn", 1, 4, "V"), ("ex", 5, 3, "S"), ("m", 6, 0, "PE"), ("bn", 1, 5, "V"),
-    ("m", 6, 1, "PE"), ("bn", 1, 6, "V"), ("m", 6, 2, "PE"), ("m", 6, 3, "PE"), ("ex", 6, 0, "S"), ("bn", 1, 7, "V"),
-    ("m", 7, 0, "PE"), ("m", 7, 1, "PE"), ("ex", 6, 1, "S"), ("qx", 5, 0, "V"), ("m", 7, 2, "PE"), ("ex", 6, 2, "S"),
-    ("m", 7, 3, "PE"), ("ex", 6, 3, "S"), ("z", 2, 0, "PE"), ("ex", 7, 0, "S"), ("z", 2, 1, "PE"), ("ex", 7, 1, "S"),
-    ("z", 2, 2, "PE"), ("qx", 6, 0, "V"), ("ex", 7, 2, "S"), ("z", 2, 3, "PE"), ("bn", 2, 0, "V"), ("ex", 7, 3, "S"),
-    ("z", 2, 4, "PE"), ("bn", 2, 1, "V"), ("z", 2, 5, "PE"), ("bn", 2, 2, "V"), ("z", 2, 6, "PE"), ("bn", 2, 3, "V"),
-    ("z", 2, 7, "PE"), ("qx", 7, 0, "V"), ("bn", 2, 4, "V"), ("bn", 2, 5, "V"), ("z", 3, 0, "PE"), ("bn", 2, 6, "V"),
-    ("z", 3, 1, "PE"), ("bn", 2, 7, "V"), ("z", 3, 2, "PE"), ("bn", 3, 0, "V"), ("z", 3, 3, "PE"), ("bn", 3, 1, "V"),
-    ("z", 3, 4, "PE"), ("bn", 3, 2, "V"), ("z", 3, 5, "PE"), ("z", 3, 6, "PE"), ("ag", 0, 0, "V"), ("bn", 3, 3, "V"),
-    ("z", 3, 7, "PE"), ("bn", 3, 4, "V"), ("sq", 0, 0, "S"), ("ag", 1, 0, "V"), ("bn", 3, 5, "V"), ("bn", 3, 6, "V"),
-    ("sq", 1, 0, "S"), ("co", 0, 0, "V"), ("ag", 2, 0, "V"), ("f", 0, 0, "PE"), ("bn", 3, 7, "V"), ("co", 1, 0, "V"),
-    ("af", 0, 3, "S"), ("ag", 3, 0, "V"), ("sq", 2, 0, "S"), ("f", 0, 1, "PE"), ("af", 1, 3, "S"), ("af", 0, 0, "S"),
-    ("f", 0, 2, "PE"), ("co", 2, 0, "V"), ("sq", 3, 0, "S"), ("af", 0, 1, "S"), ("f", 1, 0, "PE"), ("af", 5, 3, "V"),
-    ("af", 2, 3, "S"), ("f", 1, 1, "PE"), ("co", 3, 0, "V"), ("af", 3, 3, "S"), ("f", 1, 2, "PE"), ("lr", 0, 0, "V"),
-    ("af", 0, 2, "S"), ("f", 2, 0, "PE"), ("af", 1, 0, "S"), ("f", 2, 1, "PE"), ("f", 2, 2, "PE"), ("af", 4, 3, "S"),
-    ("f", 3, 0, "PE"), ("af", 1, 1, "S"), ("lr", 1, 0, "V"), ("f", 3, 1, "PE"), ("af", 1, 2, "S"), ("f", 3, 2, "PE"),
-    ("af", 2, 0, "S"), ("f", 4, 0, "PE"), ("af", 2, 1, "S"), ("f", 4, 1, "PE"), ("lr", 2, 0, "V"), ("af", 2, 2, "S"),
-    ("f", 4, 2, "PE"), ("af", 3, 0, "S"), ("f", 5, 0, "PE"), ("af", 3, 1, "S"), ("f", 5, 1, "PE"), ("af", 3, 2, "S"),
-    ("af", 4, 1, "V"), ("f", 5, 2, "PE"), ("af", 4, 0, "S"), ("lr", 3, 0, "V"), ("f", 6, 0, "PE"), ("af", 4, 2, "S"),
-    ("f", 6, 1, "PE"), ("af", 5, 0, "S"), ("f", 6, 2, "PE"), ("af", 5, 1, "S"), ("f", 6, 3, "PE"), ("lr", 4, 0, "V"),
-    ("f", 7, 0, "PE"), ("af", 5, 2, "S"), ("f", 7, 1, "PE"), ("af", 6, 0, "S"), ("f", 7, 2, "PE"), ("af", 6, 1, "S"),
-    ("f", 7, 3, "PE"), ("lr", 5, 0, "V"), ("af", 6, 2, "S"), ("af", 7, 0, "S"), ("af", 7, 1, "S"), ("af", 7, 2, "S"),
-    ("af", 6, 3, "V"), ("af", 7, 3, "S"), ("lr", 6, 0, "V"), ("lr", 7, 0, "V"), ("lr", 8, 0, "V"), ("lr", 9, 0, "V"),
+    ("mk", 0, 0, "V"), ("ab", 0, 0, "S"), ("pr", 0, 0, "V"), ("mk", 1, 0, "V"), ("qp", 0, 0, "V"), ("ab", 1, 0, "S"),
+    ("mk", 2, 0, "V"), ("sc", 0, 0, "V"), ("tr", 0, 0, "PE"), ("ab", 2, 0, "S"), ("tr", 0, 1, "PE"), ("sc", 1, 0, "V"),
+    ("wt", 0, 0, "PE"), ("wt", 0, 1, "PE"), ("ee", 0, 1, "V"), ("wt", 1, 0, "PE"), ("tr", 1, 0, "PE"), ("ee", 0, 0, "S"),
+    ("tr", 1, 1, "PE"), ("mk", 3, 0, "V"), ("pr", 1, 0, "V"), ("wt", 1, 1, "PE"), ("we", 0, 0, "S"), ("we", 0, 1, "S"),
+    ("qe", 0, 0, "V"), ("wt", 0, 2, "PE"), ("ee", 1, 0, "S"), ("wt", 0, 3, "PE"), ("sc", 2, 0, "V"), ("wt", 1, 2, "PE"),
+    ("we", 0, 2, "S"), ("ee", 1, 1, "V"), ("m", 0, 0, "PE"), ("we", 0, 3, "S"), ("m", 0, 1, "PE"), ("ex", 0, 0, "S"),
+    ("m", 0, 2, "PE"), ("qp", 1, 0, "V"), ("ex", 0, 1, "S"), ("m", 0, 3, "PE"), ("qw", 0, 0, "V"), ("wt", 1, 3, "PE"),
+    ("ex", 0, 2, "S"), ("tr", 2, 0, "PE"), ("ex", 0, 3, "S"), ("qe", 1, 0, "V"), ("tr", 2, 1, "PE"), ("we", 1, 0, "S"),
+    ("mk", 4, 0, "V"), ("we", 1, 1, "S"), ("qx", 0, 0, "V"), ("m", 1, 0, "PE"), ("we", 1, 2, "S"), ("ee", 2, 1, "V"),
+    ("m", 1, 1, "PE"), ("m", 1, 2, "PE"), ("we", 1, 3, "S"), ("m", 1, 3, "PE"), ("ab", 3, 0, "S"), ("mk", 5, 0, "V"),
+    ("pr", 2, 0, "V"), ("qw", 1, 0, "V"), ("ex", 1, 0, "S"), ("qp", 2, 0, "V"), ("ex", 1, 1, "S"), ("sc", 3, 0, "V"),
+    ("ex", 1, 2, "S"), ("ex", 1, 3, "S"), ("mk", 6, 0, "V"), ("ee", 2, 0, "S"), ("mk", 7, 0, "V"), ("pr", 3, 0, "V"),
+    ("tr", 3, 0, "PE"), ("tr", 3, 1, "PE"), ("ab", 4, 0, "S"), ("qx", 1, 0, "V"), ("qe", 2, 0, "V"), ("ee", 3, 1, "V"),
+    ("z", 0, 0, "PE"), ("m", 2, 0, "PE"), ("ee", 3, 0, "S"), ("m", 2, 1, "PE"), ("bn", 0, 0, "V"), ("m", 2, 2, "PE"),
+    ("m", 2, 3, "PE"), ("ex", 2, 0, "S"), ("z", 0, 1, "PE"), ("sc", 4, 0, "V"), ("ex", 2, 1, "S"), ("z", 0, 2, "PE"),
+    ("qe", 3, 0, "V"), ("ex", 2, 2, "S"), ("z", 0, 3, "PE"), ("bn", 0, 1, "V"), ("ex", 2, 3, "S"), ("tr", 4, 0, "PE"),
+    ("ab", 5, 0, "S"), ("bn", 0, 2, "V"), ("m", 3, 0, "PE"), ("m", 3, 1, "PE"), ("qx", 2, 0, "V"), ("m", 3, 2, "PE"),
+    ("m", 3, 3, "PE"), ("bn", 0, 3, "V"), ("tr", 4, 1, "PE"), ("qp", 3, 0, "V"), ("z", 0, 4, "PE"), ("ex", 3, 0, "S"),
+    ("ee", 4, 1, "V"), ("z", 0, 5, "PE"), ("ex", 3, 1, "S"), ("ex", 3, 2, "S"), ("z", 0, 6, "PE"), ("sc", 5, 0, "V"),
+    ("ex", 3, 3, "S"), ("z", 0, 7, "PE"), ("ee", 4, 0, "S"), ("bn", 0, 4, "V"), ("tr", 5, 0, "PE"), ("qx", 3, 0, "V"),
+    ("ab", 6, 0, "S"), ("tr", 5, 1, "PE"), ("bn", 0, 5, "V"), ("z", 1, 0, "PE"), ("qe", 4, 0, "V"), ("z", 1, 1, "PE"),
+    ("bn", 0, 6, "V"), ("z", 1, 2, "PE"), ("bn", 0, 7, "V"), ("ee", 5, 0, "S"), ("m", 4, 0, "PE"), ("m", 4, 1, "PE"),
+    ("ee", 5, 1, "V"), ("m", 4, 2, "PE"), ("ex", 4, 0, "S"), ("sc", 6, 0, "V"), ("ex", 4, 1, "S"), ("m", 4, 3, "PE"),
+    ("z", 1, 3, "PE"), ("ex", 4, 2, "S"), ("qe", 5, 0, "V"), ("z", 1, 4, "PE"), ("ex", 4, 3, "S"), ("bn", 1, 0, "V"),
+    ("ab", 7, 0, "S"), ("tr", 6, 0, "PE"), ("bn", 1, 1, "V"), ("m", 5, 0, "PE"), ("m", 5, 1, "PE"), ("qx", 4, 0, "V"),
+    ("m", 5, 2, "PE"), ("m", 5, 3, "PE"), ("bn", 1, 2, "V"), ("bn", 1, 3, "V"), ("ex", 5, 0, "S"), ("ex", 5, 1, "S"),
+    ("tr", 6, 1, "PE"), ("sc", 7, 0, "V"), ("ex", 5, 2, "S"), ("z", 1, 5, "PE"), ("bn", 1, 4, "V"), ("ex", 5, 3, "S"),
+    ("z", 1, 6, "PE"), ("ee", 6, 0, "S"), ("z", 1, 7, "PE"), ("bn", 1, 5, "V"), ("tr", 7, 0, "PE"), ("qx", 5, 0, "V"),
+    ("ee", 6, 1, "S"), ("tr", 7, 1, "PE"), ("bn", 1, 6, "V"), ("z", 2, 0, "PE"), ("bn", 1, 7, "V"), ("ee", 7, 0, "S"),
+    ("z", 2, 1, "PE"), ("qe", 6, 0, "V"), ("z", 2, 2, "PE"), ("ee", 7, 1, "S"), ("bn", 2, 0, "V"), ("z", 2, 3, "PE"),
+    ("bn", 2, 1, "V"), ("m", 6, 0, "PE"), ("m", 6, 1, "PE"), ("bn", 2, 2, "V"), ("m", 6, 2, "PE"), ("ex", 6, 0, "S"),
+    ("m", 6, 3, "PE"), ("qe", 7, 0, "V"), ("z", 2, 4, "PE"), ("ex", 6, 1, "S"), ("bn", 2, 3, "V"), ("z", 2, 5, "PE"),
+    ("ex", 6, 2, "S"), ("m", 7, 0, "PE"), ("bn", 2, 4, "V"), ("ex", 6, 3, "S"), ("m", 7, 1, "PE"), ("m", 7, 2, "PE"),
+    ("bn", 2, 5, "V"), ("ex", 7, 0, "S"), ("m", 7, 3, "PE"), ("z", 2, 6, "PE"), ("ex", 7, 1, "S"), ("qx", 6, 0, "V"),
+    ("z", 2, 7, "PE"), ("ex", 7, 2, "S"), ("bn", 2, 6, "V"), ("ex", 7, 3, "S"), ("bn", 2, 7, "V"), ("qx", 7, 0, "V"),
+    ("z", 3, 0, "PE"), ("z", 3, 1, "PE"), ("z", 3, 2, "PE"), ("bn", 3, 0, "V"), ("z", 3, 3, "PE"), ("bn", 3, 1, "V"),
+    ("z", 3, 4, "PE"), ("bn", 3, 2, "V"), ("z", 3, 5, "PE"), ("ag", 0, 0, "V"), ("z", 3, 6, "PE"), ("bn", 3, 3, "V"),
+    ("z", 3, 7, "PE"), ("sq", 0, 0, "S"), ("bn", 3, 4, "V"), ("f", 0, 0, "PE"), ("ag", 1, 0, "V"), ("f", 0, 1, "PE"),
+    ("co", 0, 0, "V"), ("f", 0, 2, "PE"), ("sq", 1, 0, "S"), ("bn", 3, 5, "V"), ("f", 0, 3, "PE"), ("af", 0, 0, "S"),
+    ("co", 1, 0, "V"), ("f", 1, 0, "PE"), ("af", 0, 1, "S"), ("f", 1, 1, "PE"), ("ag", 2, 0, "V"), ("bn", 3, 6, "V"),
+    ("af", 0, 2, "S"), ("f", 1, 2, "PE"), ("f", 1, 3, "PE"), ("bn", 3, 7, "V"), ("sq", 2, 0, "S"), ("af", 0, 3, "S"),
+    ("f", 2, 0, "PE"), ("ag", 3, 0, "V"), ("af", 1, 0, "S"), ("f", 2, 1, "PE"), ("co", 2, 0, "V"), ("af", 1, 1, "S"),
+    ("f", 2, 2, "PE"), ("lr", 0, 0, "V"), ("f", 2, 3, "PE"), ("sq", 3, 0, "S"), ("af", 1, 2, "S"), ("f", 3, 0, "PE"),
+    ("af", 1, 3, "S"), ("f", 3, 1, "PE"), ("af", 2, 0, "S"), ("f", 3, 2, "PE"), ("co", 3, 0, "V"), ("f", 3, 3, "PE"),
+    ("af", 2, 1, "S"), ("f", 4, 0, "PE"), ("lr", 1, 0, "V"), ("af", 2, 2, "S"), ("f", 4, 1, "PE"), ("af", 2, 3, "S"),
+    ("f", 4, 2, "PE"), ("af", 3, 0, "S"), ("f", 4, 3, "PE"), ("af", 3, 1, "S"), ("lr", 2, 0, "V"), ("f", 5, 0, "PE"),
+    ("af", 3, 2, "S"), ("f", 5, 1, "PE"), ("af", 3, 3, "S"), ("f", 5, 2, "PE"), ("af", 4, 0, "S"), ("f", 5, 3, "PE"),
+    ("af", 4, 1, "S"), ("lr", 3, 0, "V"), ("f", 6, 0, "PE"), ("af", 4, 2, "S"), ("f", 6, 1, "PE"), ("af", 4, 3, "S"),
+    ("f", 6, 2, "PE"), ("af", 5, 0, "S"), ("f", 6, 3, "PE"), ("af", 5, 1, "S"), ("lr", 4, 0, "V"), ("f", 7, 0, "PE"),
+    ("af", 5, 2, "S"), ("f", 7, 1, "PE"), ("af", 5, 3, "S"), ("f", 7, 2, "PE"), ("af", 6, 0, "S"), ("f", 7, 3, "PE"),
+    ("af", 6, 1, "S"), ("lr", 5, 0, "V"), ("af", 6, 2, "S"), ("af", 6, 3, "S"), ("af", 7, 0, "S"), ("lr", 6, 0, "V"),
+    ("af", 7, 1, "S"), ("af", 7, 2, "S"), ("af", 7, 3, "S"), ("lr", 7, 0, "V"), ("lr", 7, 1, "V"),
 )
-FINAL = ((0, 3), (1, 3), (0, 0), (0, 1), (2, 3), (3, 3), (0, 2), (1, 0), (4, 3), (5, 3), (1, 1), (1, 2), (2, 0), (2, 1), (2, 2), (3, 0), (3, 1), (3, 2), (4, 0), (4, 1), (4, 2), (5, 0), (5, 1), (5, 2), (6, 0), (6, 1), (6, 2), (6, 3), (7, 0), (7, 1), (7, 2), (7, 3))
-GROUP_SIZES = (4, 4, 4, 4, 4, 4, 4, 2, 1, 1)

@@ -63,7 +63,7 @@ def tile_yuyipointupdate_pa_kernel(tc, distribution_edge, instance_edge, point_n
                     nc.sync.dma_start(out=er3[i], in_=src)
             elif what[0] == "P":
                 t = raw.tile([P, 4, D], BF16, name="pr%d" % i)
-                nc.sync.dma_start(out=t[:], in_=point_node[i].rearrange("(t p) f -> p t f", p=P))
+                nc.sync.dma_start(out=t[:].rearrange("p (u e) f -> p u e f", u=2), in_=point_node[i].rearrange("(u p e) f -> p u e f", u=2, e=2))
                 pr[i] = t
             else:
                 nc.sync.dma_start(out=wr[:, 4 * i:4 * i + 4, :], in_=w_view[:, 4 * i:4 * i + 4, :])
@@ -78,16 +78,13 @@ def tile_yuyipointupdate_pa_kernel(tc, distribution_edge, instance_edge, point_n
         nc.vector.memset(eps_t[:], EPS_BN)
         junk = const.tile([P, N], BF16, name="junk")
         junk1 = const.tile([P, 1], F32, name="junk1")
+        nc.scalar.activation(out=junk1[:], in_=eps_t[:], func=ACT.Sqrt)
         st = const.tile([P, NO, B, 6], F32, name="st")
         ssum = const.tile([P, NU, 8], F32, name="ssum")
         rs = const.tile([P, NU, 8], F32, name="rs")
 
-        gps = psum.tile([P, P], BF16, name="gps", tag="ps")
-        nc.tensor.transpose(gps[:], gb[:], ident_bf[:])
         gm = const.tile([P, 2, NO], F32, name="gm")
-        nc.vector.tensor_copy(out=gm[:, 0, :], in_=gps[:, 0:NO])
         bT = const.tile([P, NO], F32, name="bT")
-        nc.vector.tensor_copy(out=bT[:], in_=gps[:, NO:2 * NO])
 
         wg = keep.tile([P, 2 * C * 4], BF16, name="wg", align_bytes=64)
         wc = keep.tile([P, 2, C], U32, name="wc", align_bytes=64)
@@ -128,30 +125,37 @@ def tile_yuyipointupdate_pa_kernel(tc, distribution_edge, instance_edge, point_n
             return z
 
         def step(kind, i, j, engine):
-            if kind == "mk":
+            if kind == "gt":
+                gps = psum.tile([P, P], BF16, name="gps", tag="ps")
+                nc.tensor.transpose(gps[:], gb[:], ident_bf[:])
+                live["gps"] = gps
+            elif kind == "ge":
+                nc.vector.tensor_copy(out=gm[:, 0, :], in_=live["gps"][:, 0:NO])
+                nc.vector.tensor_copy(out=bT[:], in_=live["gps"][:, NO:2 * NO])
+            elif kind == "mk":
                 blk = er[i][:].rearrange("p (T x) -> p T x", x=N + P)[:, :, 0:P]
                 nc.vector.tensor_tensor(out=blk, in0=blk, in1=offd[:].unsqueeze(1).to_broadcast([P, 4, P]), op=ALU.mult)
             elif kind == "ab":
                 for T in range(4):
                     nc.scalar.activation(out=junk[:], in_=er3[i][:, T, :], func=ACT.Abs, accum_out=ssum[:, i, T:T + 1])
-                if i == NU - 1:
-                    nc.scalar.activation(out=junk1[:], in_=ssum[:, i, 3:4], func=ACT.Sqrt)
             elif kind == "sc":
                 nc.vector.tensor_scalar(out=rs[:, i, 0:4], in0=ssum[:, i, 0:4], scalar1=EPS_L1, scalar2=None, op0=ALU.max)
                 nc.vector.reciprocal(out=rs[:, i, 0:4], in_=rs[:, i, 0:4])
                 for T in range(4):
                     nc.vector.tensor_scalar(out=er3[i][:, T, :], in0=er3[i][:, T, :], scalar1=rs[:, i, T:T + 1], scalar2=None, op0=ALU.mult)
             elif kind == "tr":
-                pt = psum.tile([P, 2, 4, P], BF16, name="pt", tag="ps")
+                pt = psum.tile([P, 2, 2, P], F32, name="pt", tag="ps")
+                er32 = er[i][:, 0:4 * N].bitcast(F32).rearrange("p (T w) -> p T w", T=4)
                 for Th in range(2):
-                    for k in range(4):
-                        nc.tensor.transpose(pt[:, Th, k, :], er3[i][:, 2 * j + Th, k * P:(k + 1) * P], ident_bf[:])
+                    for u in range(2):
+                        nc.tensor.transpose(pt[:, Th, u, :], er32[:, 2 * j + Th, u * P:(u + 1) * P], ident_f[:])
                 live[("pt", i, j)] = pt
             elif kind == "ee":
                 if ("eg", i) not in live:
                     live[("eg", i)] = work.tile([P, N, 4], BF16, name="eg", align_bytes=64)
-                dst = live[("eg", i)][:, 256 * j:256 * (j + 1), :].rearrange("p (T n) k -> p T n k", T=2)
-                copy_on(engine, dst, live[("pt", i, j)][:].rearrange("p T k n -> p T n k"))
+                eg32 = live[("eg", i)][:].rearrange("p n k -> p (n k)").bitcast(F32).rearrange("p (n u) -> p n u", u=2)
+                dst = eg32[:, 256 * j:256 * (j + 1), :].rearrange("p (T n) u -> p T n u", T=2)
+                copy_on(engine, dst, live[("pt", i, j)][:].rearrange("p T u n -> p T n u"))
             elif kind == "qe":
                 ec = work.tile([P, N], U32, name="ec", align_bytes=64)
                 es = work.tile([P, N], U8, name="es", align_bytes=64)
@@ -253,8 +257,8 @@ def tile_yuyipointupdate_pa_kernel(tc, distribution_edge, instance_edge, point_n
 ORDER = (
     ("mk", 0, 0, "V"), ("ab", 0, 0, "S"), ("pr", 0, 0, "V"), ("mk", 1, 0, "V"), ("qp", 0, 0, "V"), ("ab", 1, 0, "S"),
     ("mk", 2, 0, "V"), ("sc", 0, 0, "V"), ("tr", 0, 0, "PE"), ("ab", 2, 0, "S"), ("tr", 0, 1, "PE"), ("sc", 1, 0, "V"),
-    ("wt", 0, 0, "PE"), ("wt", 0, 1, "PE"), ("ee", 0, 1, "V"), ("wt", 1, 0, "PE"), ("tr", 1, 0, "PE"), ("ee", 0, 0, "S"),
-    ("tr", 1, 1, "PE"), ("mk", 3, 0, "V"), ("pr", 1, 0, "V"), ("wt", 1, 1, "PE"), ("we", 0, 0, "S"), ("we", 0, 1, "S"),
+    ("wt", 0, 0, "PE"), ("wt", 0, 1, "PE"), ("gt", 0, 0, "PE"), ("ee", 0, 1, "V"), ("wt", 1, 0, "PE"), ("tr", 1, 0, "PE"), ("ee", 0, 0, "S"),
+    ("tr", 1, 1, "PE"), ("mk", 3, 0, "V"), ("ge", 0, 0, "V"), ("pr", 1, 0, "V"), ("wt", 1, 1, "PE"), ("we", 0, 0, "S"), ("we", 0, 1, "S"),
     ("qe", 0, 0, "V"), ("wt", 0, 2, "PE"), ("ee", 1, 0, "S"), ("wt", 0, 3, "PE"), ("sc", 2, 0, "V"), ("wt", 1, 2, "PE"),
     ("we", 0, 2, "S"), ("ee", 1, 1, "V"), ("m", 0, 0, "PE"), ("we", 0, 3, "S"), ("m", 0, 1, "PE"), ("ex", 0, 0, "S"),
     ("m", 0, 2, "PE"), ("qp", 1, 0, "V"), ("ex", 0, 1, "S"), ("m", 0, 3, "PE"), ("qw", 0, 0, "V"), ("wt", 1, 3, "PE"),

@@ -9,6 +9,7 @@ U32 = mybir.dt.uint32
 U8 = mybir.dt.uint8
 FP8X4 = mybir.dt.float8_e4m3fn_x4
 ALU = mybir.AluOpType
+AX = mybir.AxisListType
 ACT = mybir.ActivationFunctionType
 
 P = 128
@@ -18,12 +19,152 @@ D = 512
 C = 1024
 NO = C // P
 NU = 2 * B
-GRP = 2
 EPS_L1 = 1e-12
 EPS_BN = 1e-5
 NEG_SLOPE = 0.01
 
 FLOPS = 2 * (2 * B * N * N * D) + 2 * B * C * C * N
+
+GROUPS = (0, 1, 3, 6, 8)
+LOADS = ("E0", "E1", "E2", "P0", "E3", "W0", "E4", "P1", "W1", "E5", "P2", "E6", "P3", "E7")
+PIECES = {0: 4, 7: 4}
+W_ORDER = ((0, 0), (0, 1), (1, 0), (1, 1), (0, 2), (0, 3), (1, 2), (1, 3))
+
+
+def inputs(s):
+    kind, i, j = s[0], s[1], s[2]
+    if kind == "a":
+        return [("mk", i, j // 2 if i == 0 else 0)]
+    if kind == "ge":
+        return [("gt", 0, 0)]
+    if kind == "rc1":
+        return [("a", i, T) for T in range(4)]
+    if kind == "rc2":
+        return [("rc1", i, 0)]
+    if kind == "sm":
+        return [("rc2", i, 0)]
+    if kind == "tr":
+        return [("sm", i, 0)]
+    if kind == "ee":
+        return [("tr", i, j)]
+    if kind == "qe":
+        return [("ee", i, 0), ("ee", i, 1)]
+    if kind == "qp":
+        return [("pr", i, 0)]
+    if kind == "m":
+        return [("qe", i, 0), ("qp", i // 2, 0)]
+    if kind == "ex":
+        return [("m", i, j)]
+    if kind == "qx":
+        return [("ex", i, k) for k in range(4)]
+    if kind == "we":
+        return [("wt", i, j)]
+    if kind == "qw":
+        return [("we", i, k) for k in range(4)]
+    if kind == "z":
+        return [("qx", 2 * i, 0), ("qx", 2 * i + 1, 0), ("qw", 0, 0), ("qw", 1, 0)]
+    if kind == "bn":
+        return [("z", i, j)]
+    if kind == "ag":
+        return [("ge", 0, 0)] + [("bn", b, O) for b in range(B) for O in range(GROUPS[i], GROUPS[i + 1])]
+    if kind == "sq":
+        return [("ag", i, 0)]
+    if kind == "c1":
+        return [("sq", i, 0)]
+    if kind == "c2":
+        return [("c1", i, 0)]
+    if kind == "c3":
+        return [("c2", i, 0)]
+    if kind == "af":
+        return [("f", i, j), ("c3", sum(1 for lo in GROUPS[1:] if lo <= i), 0)]
+    if kind == "lr":
+        w = B // PIECES.get(i, 1)
+        return [("af", i, b) for b in range(w * j, w * j + w)]
+    return []
+
+
+def queues():
+    placed = {"S": [], "V": [], "PE": [], "G": []}
+
+    def put(place, kind, i, j, engine):
+        placed[engine].append((place, len(placed[engine]), (kind, i, j, engine)))
+
+    for i in range(NU):
+        if i == 0:
+            put(-9.0, "mk", 0, 0, "V")
+            put(-9.0, "mk", 0, 1, "V")
+        else:
+            put(i - 4.75, "mk", i, 0, "V")
+        for T in range(4):
+            put(i - 3.5 + 0.1875 * T, "a", i, T, "S")
+        put(i - 2.75, "rc1", i, 0, "V")
+        put(i - 2.5, "rc2", i, 0, "V")
+        put(i - 2.25, "sm", i, 0, "V")
+        for h in range(2):
+            put(i - 1.25, "tr", i, h, "PE")
+            put(i - 1.25 + 0.125 * h, "ee", i, h, "S")
+        put(i - 1.0, "qe", i, 0, "V")
+        for j in range(4):
+            put(i + 0.0 + 0.125 * j, "m", i, j, "PE")
+            put(i + 0.25 + 0.0 * j, "ex", i, j, "S")
+        put(i + 0.5, "qx", i, 0, "V")
+    for b in range(B):
+        put(1.75 * b - 2.0, "pr", b, 0, "V")
+        put(1.75 * b - 1.5, "qp", b, 0, "V")
+    for n, (g, k) in enumerate(W_ORDER):
+        put(-0.75 + 0.25 * n, "wt", g, k, "PE")
+        put(-1.0 + 0.25 * n, "we", g, k, "S" if n == 7 else "V")
+    put(0.5, "qw", 0, 0, "V")
+    put(1.0, "qw", 1, 0, "V")
+    put(0.9, "gt", 0, 0, "PE")
+    put(1.4, "ge", 0, 0, "V")
+    for b in range(B):
+        for O in range(NO):
+            put(2 * b + 2.5 + 0.1875 * O, "z", b, O, "PE")
+            if b < B - 1:
+                put(2 * b + 2.0 + 0.25 * O, "bn", b, O, "V")
+    q = {}
+    for engine in placed:
+        q[engine] = [s for place, n, s in sorted(placed[engine])]
+
+    bn = [("bn", B - 1, O, "V") for O in range(NO)]
+    ag = [("ag", g, 0, "V") for g in range(4)]
+    c1, c2, c3 = ([(kind, g, 0, "V") for g in range(4)] for kind in ("c1", "c2", "c3"))
+    q["V"] += [bn[0], ag[0], bn[1], c1[0], bn[2], c2[0], c3[0], ag[1], bn[3], c1[1], bn[4], c2[1], bn[5], c3[1], ag[2], bn[6], bn[7]]
+    late = [ag[3], c1[2], c2[2], c3[2], c1[3], c2[3], c3[3]]
+    for O in range(NO):
+        for j in range(PIECES.get(O, 1)):
+            q["V"].append(("lr", O, j, "V"))
+            if late:
+                q["V"].append(late.pop(0))
+    last_z = q["PE"][-4:]
+    q["PE"] = q["PE"][:-4]
+    q["S"].append(("sq", 0, 0, "S"))
+    for O in range(NO):
+        for b in range(B):
+            q["PE"].append(("f", O, b, "PE"))
+            if last_z:
+                q["PE"].append(last_z.pop(0))
+            q["S"].append(("af", O, b, "S"))
+            if (O, b) in ((0, 0), (1, 0), (1, 3)):
+                q["S"].append(("sq", 1 + ((0, 0), (1, 0), (1, 3)).index((O, b)), 0, "S"))
+    return q
+
+
+def merged(q):
+    at = {engine: 0 for engine in q}
+    written = set()
+    text = []
+    while len(text) < sum(len(steps) for steps in q.values()):
+        before = len(text)
+        for engine in q:
+            while at[engine] < len(q[engine]) and all(x in written for x in inputs(q[engine][at[engine]])):
+                s = q[engine][at[engine]]
+                at[engine] += 1
+                written.add(s[:3])
+                text.append(s)
+        assert len(text) > before, "the queues wait for each other"
+    return text
 
 
 def tile_yuyipointupdate_pa_kernel(tc, distribution_edge, instance_edge, point_node, W1, g1, b1, out):
@@ -41,15 +182,9 @@ def tile_yuyipointupdate_pa_kernel(tc, distribution_edge, instance_edge, point_n
         er = {}
         er3 = {}
         pr = {}
-
-        gb = const.tile([P, P], BF16, name="gb")
-        nc.vector.memset(gb[:], 0.0)
-        nc.scalar.dma_start(out=gb[0:NO, :], in_=g1.rearrange("(o p) -> o p", p=P))
-        nc.scalar.dma_start(out=gb[NO:2 * NO, :], in_=b1.rearrange("(o p) -> o p", p=P))
-
         wr = raw.tile([P, NO, C], BF16, name="wr")
         w_view = W1.rearrange("(O p) c -> p O c", p=P)
-        for what in ("E0", "P0", "E1", "E2", "W0", "E3", "P1", "W1", "E4", "P2", "E5", "E6", "P3", "E7"):
+        for what in LOADS:
             i = int(what[1])
             if what[0] == "E":
                 t = raw.tile([P, 5 * N], BF16, name="er%d" % i)
@@ -68,24 +203,26 @@ def tile_yuyipointupdate_pa_kernel(tc, distribution_edge, instance_edge, point_n
             else:
                 nc.sync.dma_start(out=wr[:, 4 * i:4 * i + 4, :], in_=w_view[:, 4 * i:4 * i + 4, :])
 
+        eps_t = const.tile([P, 1], F32, name="eps_t")
+        nc.vector.memset(eps_t[:], EPS_BN)
+        junk1 = const.tile([P, 1], F32, name="junk1")
+        nc.scalar.activation(out=junk1[:], in_=eps_t[:], func=ACT.Sqrt)
+        gb = const.tile([P, P], BF16, name="gb")
+        nc.vector.memset(gb[:], 0.0)
+        nc.scalar.dma_start(out=gb[0:NO, :], in_=g1.rearrange("(o p) -> o p", p=P))
+        nc.scalar.dma_start(out=gb[NO:2 * NO, :], in_=b1.rearrange("(o p) -> o p", p=P))
         ident_bf = const.tile([P, P], BF16, name="ident_bf")
         make_identity(nc, ident_bf[:])
         ident_f = const.tile([P, P], F32, name="ident_f")
         make_identity(nc, ident_f[:])
         offd = const.tile([P, P], BF16, name="offd")
         nc.vector.tensor_scalar(out=offd[:], in0=ident_bf[:], scalar1=-1.0, scalar2=1.0, op0=ALU.mult, op1=ALU.add)
-        eps_t = const.tile([P, 1], F32, name="eps_t")
-        nc.vector.memset(eps_t[:], EPS_BN)
         junk = const.tile([P, N], BF16, name="junk")
-        junk1 = const.tile([P, 1], F32, name="junk1")
-        nc.scalar.activation(out=junk1[:], in_=eps_t[:], func=ACT.Sqrt)
         st = const.tile([P, NO, B, 6], F32, name="st")
         ssum = const.tile([P, NU, 8], F32, name="ssum")
         rs = const.tile([P, NU, 8], F32, name="rs")
-
         gm = const.tile([P, 2, NO], F32, name="gm")
         bT = const.tile([P, NO], F32, name="bT")
-
         wg = keep.tile([P, 2 * C * 4], BF16, name="wg", align_bytes=64)
         wc = keep.tile([P, 2, C], U32, name="wc", align_bytes=64)
         ws = keep.tile([P, 2, C], U8, name="ws", align_bytes=64)
@@ -134,13 +271,21 @@ def tile_yuyipointupdate_pa_kernel(tc, distribution_edge, instance_edge, point_n
                 nc.vector.tensor_copy(out=bT[:], in_=live["gps"][:, NO:2 * NO])
             elif kind == "mk":
                 blk = er[i][:].rearrange("p (T x) -> p T x", x=N + P)[:, :, 0:P]
-                nc.vector.tensor_tensor(out=blk, in0=blk, in1=offd[:].unsqueeze(1).to_broadcast([P, 4, P]), op=ALU.mult)
-            elif kind == "ab":
-                for T in range(4):
-                    nc.scalar.activation(out=junk[:], in_=er3[i][:, T, :], func=ACT.Abs, accum_out=ssum[:, i, T:T + 1])
-            elif kind == "sc":
+                if i == 0:
+                    blk = blk[:, 2 * j:2 * j + 2, :]
+                w = 2 if i == 0 else 4
+                eng = nc.gpsimd if engine == "G" else nc.vector
+                eng.tensor_tensor(out=blk, in0=blk, in1=offd[:].unsqueeze(1).to_broadcast([P, w, P]), op=ALU.mult)
+            elif kind == "a":
+                if engine == "V":
+                    nc.vector.tensor_reduce(out=ssum[:, i, j:j + 1], in_=er3[i][:, j, :], axis=AX.X, op=ALU.add, apply_absolute_value=True)
+                else:
+                    nc.scalar.activation(out=junk[:], in_=er3[i][:, j, :], func=ACT.Abs, accum_out=ssum[:, i, j:j + 1])
+            elif kind == "rc1":
                 nc.vector.tensor_scalar(out=rs[:, i, 0:4], in0=ssum[:, i, 0:4], scalar1=EPS_L1, scalar2=None, op0=ALU.max)
+            elif kind == "rc2":
                 nc.vector.reciprocal(out=rs[:, i, 0:4], in_=rs[:, i, 0:4])
+            elif kind == "sm":
                 for T in range(4):
                     nc.vector.tensor_scalar(out=er3[i][:, T, :], in0=er3[i][:, T, :], scalar1=rs[:, i, T:T + 1], scalar2=None, op0=ALU.mult)
             elif kind == "tr":
@@ -162,11 +307,15 @@ def tile_yuyipointupdate_pa_kernel(tc, distribution_edge, instance_edge, point_n
                 nc.vector.quantize_mx(out=ec[:].bitcast(FP8X4), scales=es[:], in_=live[("eg", i)][:].rearrange("p n k -> p (n k)"))
                 live[("ec", i)] = (ec, es)
             elif kind == "pr":
-                png = work.tile([P, D, 4], BF16, name="png", align_bytes=64, bufs=2)
+                png = work.tile([P, D, 4], BF16, name="png", align_bytes=64, bufs=4)
                 dst = png[:].rearrange("q (u e p) t -> q u e p t", u=2, e=2)
                 src = pr[i][:].rearrange("q t (u p e) -> q u e p t", u=2, e=2)
                 for u in range(2):
-                    nc.vector.tensor_copy(out=dst[:, u], in_=src[:, u])
+                    if engine == "G":
+                        for e in range(2):
+                            nc.gpsimd.tensor_scalar(out=dst[:, u, e], in0=src[:, u, e], scalar1=1.0, scalar2=0.0, op0=ALU.mult, op1=ALU.add)
+                    else:
+                        nc.vector.tensor_copy(out=dst[:, u], in_=src[:, u])
                 live[("png", i)] = png
             elif kind == "qp":
                 pc[i] = keep.tile([P, D], U32, name="pc%d" % i, align_bytes=64)
@@ -216,95 +365,41 @@ def tile_yuyipointupdate_pa_kernel(tc, distribution_edge, instance_edge, point_n
             elif kind == "bn":
                 nc.vector.bn_stats(out=st[:, j, i, :], in_=live[("z", i, j)][:])
             elif kind == "ag":
-                lo, hi = GRP * i, GRP * (i + 1)
+                lo, hi = GROUPS[i], GROUPS[i + 1]
                 for O in range(lo, hi):
                     nc.vector.bn_aggr(out=mv[:, O, :], in_=st[:, O, :, :].rearrange("p b s -> p (b s)"))
-                nc.vector.tensor_tensor(out=gm[:, 1, lo:hi], in0=mv[:, lo:hi, 0], in1=gm[:, 0, lo:hi], op=ALU.mult)
+                nc.vector.scalar_tensor_tensor(out=gm[:, 1, lo:hi], in0=mv[:, lo:hi, 0], scalar=-1.0, in1=gm[:, 0, lo:hi], op0=ALU.mult, op1=ALU.mult)
             elif kind == "sq":
-                lo, hi = GRP * i, GRP * (i + 1)
+                lo, hi = GROUPS[i], GROUPS[i + 1]
                 nc.scalar.activation(out=sd[:, lo:hi], in_=mv[:, lo:hi, 1], func=ACT.Sqrt, bias=eps_t[:, 0:1], scale=1.0)
-            elif kind == "co":
-                lo, hi = GRP * i, GRP * (i + 1)
+            elif kind == "c1":
+                lo, hi = GROUPS[i], GROUPS[i + 1]
                 nc.vector.reciprocal(out=rstd[:, lo:hi], in_=sd[:, lo:hi])
-                nc.vector.tensor_tensor(out=cc[:, :, lo:hi], in0=gm[:, :, lo:hi], in1=rstd[:, lo:hi].unsqueeze(1).to_broadcast([P, 2, GRP]), op=ALU.mult)
-                nc.vector.tensor_tensor(out=cb[:, lo:hi], in0=bT[:, lo:hi], in1=cc[:, 1, lo:hi], op=ALU.subtract)
+            elif kind == "c2":
+                lo, hi = GROUPS[i], GROUPS[i + 1]
+                nc.vector.tensor_tensor(out=cc[:, :, lo:hi], in0=gm[:, :, lo:hi], in1=rstd[:, lo:hi].unsqueeze(1).to_broadcast([P, 2, hi - lo]), op=ALU.mult)
+            elif kind == "c3":
+                lo, hi = GROUPS[i], GROUPS[i + 1]
+                if hi - lo == 1:
+                    nc.vector.scalar_tensor_tensor(out=cb[:, lo:hi], in0=gm[:, 1, lo:hi], scalar=rstd[:, lo:hi], in1=bT[:, lo:hi], op0=ALU.mult, op1=ALU.add)
+                else:
+                    nc.vector.tensor_tensor(out=cb[:, lo:hi], in0=bT[:, lo:hi], in1=cc[:, 1, lo:hi], op=ALU.add)
             elif kind == "f":
                 live[("f", i, j)] = z_bank(i, j)
             elif kind == "af":
                 if ("y", i) not in live:
                     live[("y", i)] = ypool.tile([P, B, N], F32, name="y")
-                y = live[("y", i)]
-                z = live[("f", i, j)]
-                if engine == "V":
-                    nc.vector.tensor_scalar(out=y[:, j, :], in0=z[:], scalar1=cc[:, 0, i:i + 1], scalar2=cb[:, i:i + 1], op0=ALU.mult, op1=ALU.add)
-                else:
-                    nc.scalar.activation(out=y[:, j, :], in_=z[:], func=ACT.Identity, bias=cb[:, i:i + 1], scale=cc[:, 0, i:i + 1])
+                nc.scalar.activation(out=live[("y", i)][:, j, :], in_=live[("f", i, j)][:], func=ACT.Identity, bias=cb[:, i:i + 1], scale=cc[:, 0, i:i + 1])
             elif kind == "lr":
                 y = live[("y", i)]
                 if ("yo", i) not in live:
                     live[("yo", i)] = ypool.tile([P, B, N], F32, name="yo")
                 yo = live[("yo", i)]
-                width = B // (2 if i == NO - 1 else 1)
+                width = B // PIECES.get(i, 1)
                 bs = slice(j * width, (j + 1) * width)
                 yf = y[:, bs, :].rearrange("p b n -> p (b n)")
                 nc.vector.scalar_tensor_tensor(out=yo[:, bs, :].rearrange("p b n -> p (b n)"), in0=yf, scalar=NEG_SLOPE, in1=yf, op0=ALU.mult, op1=ALU.max)
                 nc.sync.dma_start(out=out_view[i][:, bs, :], in_=yo[:, bs, :])
 
-        for kind, i, j, engine in ORDER:
+        for kind, i, j, engine in merged(queues()):
             step(kind, i, j, engine)
-
-
-ORDER = (
-    ("mk", 0, 0, "V"), ("ab", 0, 0, "S"), ("pr", 0, 0, "V"), ("mk", 1, 0, "V"), ("qp", 0, 0, "V"), ("ab", 1, 0, "S"),
-    ("mk", 2, 0, "V"), ("sc", 0, 0, "V"), ("tr", 0, 0, "PE"), ("ab", 2, 0, "S"), ("tr", 0, 1, "PE"), ("sc", 1, 0, "V"),
-    ("wt", 0, 0, "PE"), ("wt", 0, 1, "PE"), ("gt", 0, 0, "PE"), ("ee", 0, 1, "V"), ("wt", 1, 0, "PE"), ("tr", 1, 0, "PE"), ("ee", 0, 0, "S"),
-    ("tr", 1, 1, "PE"), ("mk", 3, 0, "V"), ("ge", 0, 0, "V"), ("pr", 1, 0, "V"), ("wt", 1, 1, "PE"), ("we", 0, 0, "S"), ("we", 0, 1, "S"),
-    ("qe", 0, 0, "V"), ("wt", 0, 2, "PE"), ("ee", 1, 0, "S"), ("wt", 0, 3, "PE"), ("sc", 2, 0, "V"), ("wt", 1, 2, "PE"),
-    ("we", 0, 2, "S"), ("ee", 1, 1, "V"), ("m", 0, 0, "PE"), ("we", 0, 3, "S"), ("m", 0, 1, "PE"), ("ex", 0, 0, "S"),
-    ("m", 0, 2, "PE"), ("qp", 1, 0, "V"), ("ex", 0, 1, "S"), ("m", 0, 3, "PE"), ("qw", 0, 0, "V"), ("wt", 1, 3, "PE"),
-    ("ex", 0, 2, "S"), ("tr", 2, 0, "PE"), ("ex", 0, 3, "S"), ("qe", 1, 0, "V"), ("tr", 2, 1, "PE"), ("we", 1, 0, "S"),
-    ("mk", 4, 0, "V"), ("we", 1, 1, "S"), ("qx", 0, 0, "V"), ("m", 1, 0, "PE"), ("we", 1, 2, "S"), ("ee", 2, 1, "V"),
-    ("m", 1, 1, "PE"), ("m", 1, 2, "PE"), ("we", 1, 3, "S"), ("m", 1, 3, "PE"), ("ab", 3, 0, "S"), ("mk", 5, 0, "V"),
-    ("pr", 2, 0, "V"), ("qw", 1, 0, "V"), ("ex", 1, 0, "S"), ("qp", 2, 0, "V"), ("ex", 1, 1, "S"), ("sc", 3, 0, "V"),
-    ("ex", 1, 2, "S"), ("ex", 1, 3, "S"), ("mk", 6, 0, "V"), ("ee", 2, 0, "S"), ("mk", 7, 0, "V"), ("pr", 3, 0, "V"),
-    ("tr", 3, 0, "PE"), ("tr", 3, 1, "PE"), ("ab", 4, 0, "S"), ("qx", 1, 0, "V"), ("qe", 2, 0, "V"), ("ee", 3, 1, "V"),
-    ("z", 0, 0, "PE"), ("m", 2, 0, "PE"), ("ee", 3, 0, "S"), ("m", 2, 1, "PE"), ("bn", 0, 0, "V"), ("m", 2, 2, "PE"),
-    ("m", 2, 3, "PE"), ("ex", 2, 0, "S"), ("z", 0, 1, "PE"), ("sc", 4, 0, "V"), ("ex", 2, 1, "S"), ("z", 0, 2, "PE"),
-    ("qe", 3, 0, "V"), ("ex", 2, 2, "S"), ("z", 0, 3, "PE"), ("bn", 0, 1, "V"), ("ex", 2, 3, "S"), ("tr", 4, 0, "PE"),
-    ("ab", 5, 0, "S"), ("bn", 0, 2, "V"), ("m", 3, 0, "PE"), ("m", 3, 1, "PE"), ("qx", 2, 0, "V"), ("m", 3, 2, "PE"),
-    ("m", 3, 3, "PE"), ("bn", 0, 3, "V"), ("tr", 4, 1, "PE"), ("qp", 3, 0, "V"), ("z", 0, 4, "PE"), ("ex", 3, 0, "S"),
-    ("ee", 4, 1, "V"), ("z", 0, 5, "PE"), ("ex", 3, 1, "S"), ("ex", 3, 2, "S"), ("z", 0, 6, "PE"), ("sc", 5, 0, "V"),
-    ("ex", 3, 3, "S"), ("z", 0, 7, "PE"), ("ee", 4, 0, "S"), ("bn", 0, 4, "V"), ("tr", 5, 0, "PE"), ("qx", 3, 0, "V"),
-    ("ab", 6, 0, "S"), ("tr", 5, 1, "PE"), ("bn", 0, 5, "V"), ("z", 1, 0, "PE"), ("qe", 4, 0, "V"), ("z", 1, 1, "PE"),
-    ("bn", 0, 6, "V"), ("z", 1, 2, "PE"), ("bn", 0, 7, "V"), ("ee", 5, 0, "S"), ("m", 4, 0, "PE"), ("m", 4, 1, "PE"),
-    ("ee", 5, 1, "V"), ("m", 4, 2, "PE"), ("ex", 4, 0, "S"), ("sc", 6, 0, "V"), ("ex", 4, 1, "S"), ("m", 4, 3, "PE"),
-    ("z", 1, 3, "PE"), ("ex", 4, 2, "S"), ("qe", 5, 0, "V"), ("z", 1, 4, "PE"), ("ex", 4, 3, "S"), ("bn", 1, 0, "V"),
-    ("ab", 7, 0, "S"), ("tr", 6, 0, "PE"), ("bn", 1, 1, "V"), ("m", 5, 0, "PE"), ("m", 5, 1, "PE"), ("qx", 4, 0, "V"),
-    ("m", 5, 2, "PE"), ("m", 5, 3, "PE"), ("bn", 1, 2, "V"), ("bn", 1, 3, "V"), ("ex", 5, 0, "S"), ("ex", 5, 1, "S"),
-    ("tr", 6, 1, "PE"), ("sc", 7, 0, "V"), ("ex", 5, 2, "S"), ("z", 1, 5, "PE"), ("bn", 1, 4, "V"), ("ex", 5, 3, "S"),
-    ("z", 1, 6, "PE"), ("ee", 6, 0, "S"), ("z", 1, 7, "PE"), ("bn", 1, 5, "V"), ("tr", 7, 0, "PE"), ("qx", 5, 0, "V"),
-    ("ee", 6, 1, "S"), ("tr", 7, 1, "PE"), ("bn", 1, 6, "V"), ("z", 2, 0, "PE"), ("bn", 1, 7, "V"), ("ee", 7, 0, "S"),
-    ("z", 2, 1, "PE"), ("qe", 6, 0, "V"), ("z", 2, 2, "PE"), ("ee", 7, 1, "S"), ("bn", 2, 0, "V"), ("z", 2, 3, "PE"),
-    ("bn", 2, 1, "V"), ("m", 6, 0, "PE"), ("m", 6, 1, "PE"), ("bn", 2, 2, "V"), ("m", 6, 2, "PE"), ("ex", 6, 0, "S"),
-    ("m", 6, 3, "PE"), ("qe", 7, 0, "V"), ("z", 2, 4, "PE"), ("ex", 6, 1, "S"), ("bn", 2, 3, "V"), ("z", 2, 5, "PE"),
-    ("ex", 6, 2, "S"), ("m", 7, 0, "PE"), ("bn", 2, 4, "V"), ("ex", 6, 3, "S"), ("m", 7, 1, "PE"), ("m", 7, 2, "PE"),
-    ("bn", 2, 5, "V"), ("ex", 7, 0, "S"), ("m", 7, 3, "PE"), ("z", 2, 6, "PE"), ("ex", 7, 1, "S"), ("qx", 6, 0, "V"),
-    ("z", 2, 7, "PE"), ("ex", 7, 2, "S"), ("bn", 2, 6, "V"), ("ex", 7, 3, "S"), ("bn", 2, 7, "V"), ("qx", 7, 0, "V"),
-    ("z", 3, 0, "PE"), ("z", 3, 1, "PE"), ("z", 3, 2, "PE"), ("bn", 3, 0, "V"), ("z", 3, 3, "PE"), ("bn", 3, 1, "V"),
-    ("z", 3, 4, "PE"), ("bn", 3, 2, "V"), ("z", 3, 5, "PE"), ("ag", 0, 0, "V"), ("z", 3, 6, "PE"), ("bn", 3, 3, "V"),
-    ("z", 3, 7, "PE"), ("sq", 0, 0, "S"), ("bn", 3, 4, "V"), ("f", 0, 0, "PE"), ("ag", 1, 0, "V"), ("f", 0, 1, "PE"),
-    ("co", 0, 0, "V"), ("f", 0, 2, "PE"), ("sq", 1, 0, "S"), ("bn", 3, 5, "V"), ("f", 0, 3, "PE"), ("af", 0, 0, "S"),
-    ("co", 1, 0, "V"), ("f", 1, 0, "PE"), ("af", 0, 1, "S"), ("f", 1, 1, "PE"), ("ag", 2, 0, "V"), ("bn", 3, 6, "V"),
-    ("af", 0, 2, "S"), ("f", 1, 2, "PE"), ("f", 1, 3, "PE"), ("bn", 3, 7, "V"), ("sq", 2, 0, "S"), ("af", 0, 3, "S"),
-    ("f", 2, 0, "PE"), ("ag", 3, 0, "V"), ("af", 1, 0, "S"), ("f", 2, 1, "PE"), ("co", 2, 0, "V"), ("af", 1, 1, "S"),
-    ("f", 2, 2, "PE"), ("lr", 0, 0, "V"), ("f", 2, 3, "PE"), ("sq", 3, 0, "S"), ("af", 1, 2, "S"), ("f", 3, 0, "PE"),
-    ("af", 1, 3, "S"), ("f", 3, 1, "PE"), ("af", 2, 0, "S"), ("f", 3, 2, "PE"), ("co", 3, 0, "V"), ("f", 3, 3, "PE"),
-    ("af", 2, 1, "S"), ("f", 4, 0, "PE"), ("lr", 1, 0, "V"), ("af", 2, 2, "S"), ("f", 4, 1, "PE"), ("af", 2, 3, "S"),
-    ("f", 4, 2, "PE"), ("af", 3, 0, "S"), ("f", 4, 3, "PE"), ("af", 3, 1, "S"), ("lr", 2, 0, "V"), ("f", 5, 0, "PE"),
-    ("af", 3, 2, "S"), ("f", 5, 1, "PE"), ("af", 3, 3, "S"), ("f", 5, 2, "PE"), ("af", 4, 0, "S"), ("f", 5, 3, "PE"),
-    ("af", 4, 1, "S"), ("lr", 3, 0, "V"), ("f", 6, 0, "PE"), ("af", 4, 2, "S"), ("f", 6, 1, "PE"), ("af", 4, 3, "S"),
-    ("f", 6, 2, "PE"), ("af", 5, 0, "S"), ("f", 6, 3, "PE"), ("af", 5, 1, "S"), ("lr", 4, 0, "V"), ("f", 7, 0, "PE"),
-    ("af", 5, 2, "S"), ("f", 7, 1, "PE"), ("af", 5, 3, "S"), ("f", 7, 2, "PE"), ("af", 6, 0, "S"), ("f", 7, 3, "PE"),
-    ("af", 6, 1, "S"), ("lr", 5, 0, "V"), ("af", 6, 2, "S"), ("af", 6, 3, "S"), ("af", 7, 0, "S"), ("lr", 6, 0, "V"),
-    ("af", 7, 1, "S"), ("af", 7, 2, "S"), ("af", 7, 3, "S"), ("lr", 7, 0, "V"), ("lr", 7, 1, "V"),
-)

from contextlib import ExitStack

import concourse.mybir as mybir
from concourse.masks import make_identity

F32 = mybir.dt.float32
BF16 = mybir.dt.bfloat16
U32 = mybir.dt.uint32
U8 = mybir.dt.uint8
FP8X4 = mybir.dt.float8_e4m3fn_x4
ALU = mybir.AluOpType
AX = mybir.AxisListType
ACT = mybir.ActivationFunctionType

P = 128
B = 4
N = 512
D = 512
C = 1024
NO = C // P
NU = 2 * B
EPS_L1 = 1e-12
EPS_BN = 1e-5
NEG_SLOPE = 0.01

FLOPS = 2 * (2 * B * N * N * D) + 2 * B * C * C * N

GROUPS = (0, 1, 3, 6, 8)
LOADS = ("E0", "E1", "E2", "P0", "E3", "W0", "E4", "P1", "W1", "E5", "P2", "E6", "P3", "E7")
PIECES = {0: 4, 7: 4}
W_ORDER = ((0, 0), (0, 1), (1, 0), (1, 1), (0, 2), (0, 3), (1, 2), (1, 3))


def inputs(s):
    kind, i, j = s[0], s[1], s[2]
    if kind == "a":
        return [("mk", i, j // 2 if i == 0 else 0)]
    if kind == "ge":
        return [("gt", 0, 0)]
    if kind == "rc1":
        return [("a", i, T) for T in range(4)]
    if kind == "rc2":
        return [("rc1", i, 0)]
    if kind == "sm":
        return [("rc2", i, 0)]
    if kind == "tr":
        return [("sm", i, 0)]
    if kind == "ee":
        return [("tr", i, j)]
    if kind == "qe":
        return [("ee", i, 0), ("ee", i, 1)]
    if kind == "qp":
        return [("pr", i, 0)]
    if kind == "m":
        return [("qe", i, 0), ("qp", i // 2, 0)]
    if kind == "ex":
        return [("m", i, j)]
    if kind == "qx":
        return [("ex", i, k) for k in range(4)]
    if kind == "we":
        return [("wt", i, j)]
    if kind == "qw":
        return [("we", i, k) for k in range(4)]
    if kind == "z":
        return [("qx", 2 * i, 0), ("qx", 2 * i + 1, 0), ("qw", 0, 0), ("qw", 1, 0)]
    if kind == "bn":
        return [("z", i, j)]
    if kind == "ag":
        return [("ge", 0, 0)] + [("bn", b, O) for b in range(B) for O in range(GROUPS[i], GROUPS[i + 1])]
    if kind == "sq":
        return [("ag", i, 0)]
    if kind == "c1":
        return [("sq", i, 0)]
    if kind == "c2":
        return [("c1", i, 0)]
    if kind == "c3":
        return [("c2", i, 0)]
    if kind == "af":
        return [("f", i, j), ("c3", sum(1 for lo in GROUPS[1:] if lo <= i), 0)]
    if kind == "lr":
        w = B // PIECES.get(i, 1)
        return [("af", i, b) for b in range(w * j, w * j + w)]
    return []


def queues():
    placed = {"S": [], "V": [], "PE": [], "G": []}

    def put(place, kind, i, j, engine):
        placed[engine].append((place, len(placed[engine]), (kind, i, j, engine)))

    for i in range(NU):
        if i == 0:
            put(-9.0, "mk", 0, 0, "V")
            put(-9.0, "mk", 0, 1, "V")
        else:
            put(i - 4.75, "mk", i, 0, "V")
        for T in range(4):
            put(i - 3.5 + 0.1875 * T, "a", i, T, "S")
        put(i - 2.75, "rc1", i, 0, "V")
        put(i - 2.5, "rc2", i, 0, "V")
        put(i - 2.25, "sm", i, 0, "V")
        for h in range(2):
            put(i - 1.25, "tr", i, h, "PE")
            put(i - 1.25 + 0.125 * h, "ee", i, h, "S")
        put(i - 1.0, "qe", i, 0, "V")
        for j in range(4):
            put(i + 0.0 + 0.125 * j, "m", i, j, "PE")
            put(i + 0.25 + 0.0 * j, "ex", i, j, "S")
        put(i + 0.5, "qx", i, 0, "V")
    for b in range(B):
        put(1.75 * b - 2.0, "pr", b, 0, "V")
        put(1.75 * b - 1.5, "qp", b, 0, "V")
    for n, (g, k) in enumerate(W_ORDER):
        put(-0.75 + 0.25 * n, "wt", g, k, "PE")
        put(-1.0 + 0.25 * n, "we", g, k, "S" if n == 7 else "V")
    put(0.5, "qw", 0, 0, "V")
    put(1.0, "qw", 1, 0, "V")
    put(0.9, "gt", 0, 0, "PE")
    put(1.4, "ge", 0, 0, "V")
    for b in range(B):
        for O in range(NO):
            put(2 * b + 2.5 + 0.1875 * O, "z", b, O, "PE")
            if b < B - 1:
                put(2 * b + 2.0 + 0.25 * O, "bn", b, O, "V")
    q = {}
    for engine in placed:
        q[engine] = [s for place, n, s in sorted(placed[engine])]

    bn = [("bn", B - 1, O, "V") for O in range(NO)]
    ag = [("ag", g, 0, "V") for g in range(4)]
    c1, c2, c3 = ([(kind, g, 0, "V") for g in range(4)] for kind in ("c1", "c2", "c3"))
    q["V"] += [bn[0], ag[0], bn[1], c1[0], bn[2], c2[0], c3[0], ag[1], bn[3], c1[1], bn[4], c2[1], bn[5], c3[1], ag[2], bn[6], bn[7]]
    late = [ag[3], c1[2], c2[2], c3[2], c1[3], c2[3], c3[3]]
    for O in range(NO):
        for j in range(PIECES.get(O, 1)):
            q["V"].append(("lr", O, j, "V"))
            if late:
                q["V"].append(late.pop(0))
    last_z = q["PE"][-4:]
    q["PE"] = q["PE"][:-4]
    q["S"].append(("sq", 0, 0, "S"))
    for O in range(NO):
        for b in range(B):
            q["PE"].append(("f", O, b, "PE"))
            if last_z:
                q["PE"].append(last_z.pop(0))
            q["S"].append(("af", O, b, "S"))
            if (O, b) in ((0, 0), (1, 0), (1, 3)):
                q["S"].append(("sq", 1 + ((0, 0), (1, 0), (1, 3)).index((O, b)), 0, "S"))
    return q


def merged(q):
    at = {engine: 0 for engine in q}
    written = set()
    text = []
    while len(text) < sum(len(steps) for steps in q.values()):
        before = len(text)
        for engine in q:
            while at[engine] < len(q[engine]) and all(x in written for x in inputs(q[engine][at[engine]])):
                s = q[engine][at[engine]]
                at[engine] += 1
                written.add(s[:3])
                text.append(s)
        assert len(text) > before, "the queues wait for each other"
    return text


def tile_yuyipointupdate_pa_kernel(tc, distribution_edge, instance_edge, point_node, W1, g1, b1, out):
    nc = tc.nc
    edges = (distribution_edge, instance_edge)
    with ExitStack() as ctx:
        const = ctx.enter_context(tc.tile_pool(name="const", bufs=1))
        raw = ctx.enter_context(tc.tile_pool(name="raw", bufs=1))
        keep = ctx.enter_context(tc.tile_pool(name="keep", bufs=1))
        work = ctx.enter_context(tc.tile_pool(name="work", bufs=3))
        ypool = ctx.enter_context(tc.tile_pool(name="ypool", bufs=3))
        psum = ctx.enter_context(tc.psum_pool(name="psum", bufs=8))
        ctx.enter_context(tc.manual_schedule())

        er = {}
        er3 = {}
        pr = {}
        wr = raw.tile([P, NO, C], BF16, name="wr")
        w_view = W1.rearrange("(O p) c -> p O c", p=P)
        for what in LOADS:
            i = int(what[1])
            if what[0] == "E":
                t = raw.tile([P, 5 * N], BF16, name="er%d" % i)
                er[i] = t
                er3[i] = t[:, 0:4 * N].rearrange("p (T m) -> p T m", T=4)
                src = edges[i % 2][i // 2].rearrange("(T p) m -> p T m", p=P)
                if i == 0:
                    nc.sync.dma_start(out=er3[i][:, 0:2, :], in_=src[:, 0:2, :])
                    nc.sync.dma_start(out=er3[i][:, 2:4, :], in_=src[:, 2:4, :])
                else:
                    nc.sync.dma_start(out=er3[i], in_=src)
            elif what[0] == "P":
                t = raw.tile([P, 4, D], BF16, name="pr%d" % i)
                nc.sync.dma_start(out=t[:].rearrange("p (u e) f -> p u e f", u=2), in_=point_node[i].rearrange("(u p e) f -> p u e f", u=2, e=2))
                pr[i] = t
            else:
                nc.sync.dma_start(out=wr[:, 4 * i:4 * i + 4, :], in_=w_view[:, 4 * i:4 * i + 4, :])

        eps_t = const.tile([P, 1], F32, name="eps_t")
        nc.vector.memset(eps_t[:], EPS_BN)
        junk1 = const.tile([P, 1], F32, name="junk1")
        nc.scalar.activation(out=junk1[:], in_=eps_t[:], func=ACT.Sqrt)
        gb = const.tile([P, P], BF16, name="gb")
        nc.vector.memset(gb[:], 0.0)
        nc.scalar.dma_start(out=gb[0:NO, :], in_=g1.rearrange("(o p) -> o p", p=P))
        nc.scalar.dma_start(out=gb[NO:2 * NO, :], in_=b1.rearrange("(o p) -> o p", p=P))
        ident_bf = const.tile([P, P], BF16, name="ident_bf")
        make_identity(nc, ident_bf[:])
        ident_f = const.tile([P, P], F32, name="ident_f")
        make_identity(nc, ident_f[:])
        offd = const.tile([P, P], BF16, name="offd")
        nc.vector.tensor_scalar(out=offd[:], in0=ident_bf[:], scalar1=-1.0, scalar2=1.0, op0=ALU.mult, op1=ALU.add)
        junk = const.tile([P, N], BF16, name="junk")
        st = const.tile([P, NO, B, 6], F32, name="st")
        ssum = const.tile([P, NU, 8], F32, name="ssum")
        rs = const.tile([P, NU, 8], F32, name="rs")
        gm = const.tile([P, 2, NO], F32, name="gm")
        bT = const.tile([P, NO], F32, name="bT")
        wg = keep.tile([P, 2 * C * 4], BF16, name="wg", align_bytes=64)
        wc = keep.tile([P, 2, C], U32, name="wc", align_bytes=64)
        ws = keep.tile([P, 2, C], U8, name="ws", align_bytes=64)
        wg32 = wg[:].bitcast(F32).rearrange("p (g o u) -> p g o u", g=2, u=2)
        mv = const.tile([P, NO, 2], F32, name="mv")
        sd = const.tile([P, NO], F32, name="sd")
        rstd = const.tile([P, NO], F32, name="rstd")
        cc = const.tile([P, 2, NO], F32, name="cc")
        cb = const.tile([P, NO], F32, name="cb")
        out_view = out.rearrange("b (O p) n -> O p b n", p=P)

        pc = {}
        ps = {}
        xc = {}
        xs = {}
        live = {}

        def copy_on(engine, dst, src):
            if engine == "S":
                nc.scalar.copy(out=dst, in_=src)
            else:
                nc.vector.tensor_copy(out=dst, in_=src)

        def z_bank(O, b):
            z = psum.tile([P, N], F32, name="z", tag="ps")
            oc = slice(O * P, (O + 1) * P)
            for g in range(2):
                nc.tensor.matmul_mx(
                    out=z[:],
                    lhsT=wc[:, g, oc].bitcast(FP8X4),
                    lhsT_scale=ws[:, g, oc],
                    rhs=xc[b][:, g, :].bitcast(FP8X4),
                    rhs_scale=xs[b][:, g, :],
                    start=(g == 0),
                    stop=(g == 1),
                )
            return z

        def step(kind, i, j, engine):
            if kind == "gt":
                gps = psum.tile([P, P], BF16, name="gps", tag="ps")
                nc.tensor.transpose(gps[:], gb[:], ident_bf[:])
                live["gps"] = gps
            elif kind == "ge":
                nc.vector.tensor_copy(out=gm[:, 0, :], in_=live["gps"][:, 0:NO])
                nc.vector.tensor_copy(out=bT[:], in_=live["gps"][:, NO:2 * NO])
            elif kind == "mk":
                blk = er[i][:].rearrange("p (T x) -> p T x", x=N + P)[:, :, 0:P]
                if i == 0:
                    blk = blk[:, 2 * j:2 * j + 2, :]
                w = 2 if i == 0 else 4
                eng = nc.gpsimd if engine == "G" else nc.vector
                eng.tensor_tensor(out=blk, in0=blk, in1=offd[:].unsqueeze(1).to_broadcast([P, w, P]), op=ALU.mult)
            elif kind == "a":
                if engine == "V":
                    nc.vector.tensor_reduce(out=ssum[:, i, j:j + 1], in_=er3[i][:, j, :], axis=AX.X, op=ALU.add, apply_absolute_value=True)
                else:
                    nc.scalar.activation(out=junk[:], in_=er3[i][:, j, :], func=ACT.Abs, accum_out=ssum[:, i, j:j + 1])
            elif kind == "rc1":
                nc.vector.tensor_scalar(out=rs[:, i, 0:4], in0=ssum[:, i, 0:4], scalar1=EPS_L1, scalar2=None, op0=ALU.max)
            elif kind == "rc2":
                nc.vector.reciprocal(out=rs[:, i, 0:4], in_=rs[:, i, 0:4])
            elif kind == "sm":
                for T in range(4):
                    nc.vector.tensor_scalar(out=er3[i][:, T, :], in0=er3[i][:, T, :], scalar1=rs[:, i, T:T + 1], scalar2=None, op0=ALU.mult)
            elif kind == "tr":
                pt = psum.tile([P, 2, 2, P], F32, name="pt", tag="ps")
                er32 = er[i][:, 0:4 * N].bitcast(F32).rearrange("p (T w) -> p T w", T=4)
                for Th in range(2):
                    for u in range(2):
                        nc.tensor.transpose(pt[:, Th, u, :], er32[:, 2 * j + Th, u * P:(u + 1) * P], ident_f[:])
                live[("pt", i, j)] = pt
            elif kind == "ee":
                if ("eg", i) not in live:
                    live[("eg", i)] = work.tile([P, N, 4], BF16, name="eg", align_bytes=64)
                eg32 = live[("eg", i)][:].rearrange("p n k -> p (n k)").bitcast(F32).rearrange("p (n u) -> p n u", u=2)
                dst = eg32[:, 256 * j:256 * (j + 1), :].rearrange("p (T n) u -> p T n u", T=2)
                copy_on(engine, dst, live[("pt", i, j)][:].rearrange("p T u n -> p T n u"))
            elif kind == "qe":
                ec = work.tile([P, N], U32, name="ec", align_bytes=64)
                es = work.tile([P, N], U8, name="es", align_bytes=64)
                nc.vector.quantize_mx(out=ec[:].bitcast(FP8X4), scales=es[:], in_=live[("eg", i)][:].rearrange("p n k -> p (n k)"))
                live[("ec", i)] = (ec, es)
            elif kind == "pr":
                png = work.tile([P, D, 4], BF16, name="png", align_bytes=64, bufs=4)
                dst = png[:].rearrange("q (u e p) t -> q u e p t", u=2, e=2)
                src = pr[i][:].rearrange("q t (u p e) -> q u e p t", u=2, e=2)
                for u in range(2):
                    if engine == "G":
                        for e in range(2):
                            nc.gpsimd.tensor_scalar(out=dst[:, u, e], in0=src[:, u, e], scalar1=1.0, scalar2=0.0, op0=ALU.mult, op1=ALU.add)
                    else:
                        nc.vector.tensor_copy(out=dst[:, u], in_=src[:, u])
                live[("png", i)] = png
            elif kind == "qp":
                pc[i] = keep.tile([P, D], U32, name="pc%d" % i, align_bytes=64)
                ps[i] = keep.tile([P, D], U8, name="ps%d" % i, align_bytes=64)
                nc.vector.quantize_mx(out=pc[i][:].bitcast(FP8X4), scales=ps[i][:], in_=live[("png", i)][:].rearrange("q c t -> q (c t)"))
                xc[i] = keep.tile([P, 2, N], U32, name="xc%d" % i, align_bytes=64)
                xs[i] = keep.tile([P, 2, N], U8, name="xs%d" % i, align_bytes=64)
            elif kind == "m":
                b = i // 2
                ec, es = live[("ec", i)]
                cols = slice(j * P, (j + 1) * P)
                ap = psum.tile([P, 4, P], F32, name="ap", tag="ps")
                for k in range(4):
                    fc = slice(k * P, (k + 1) * P)
                    nc.tensor.matmul_mx(
                        out=ap[:, k, :],
                        lhsT=pc[b][:, fc].bitcast(FP8X4),
                        lhsT_scale=ps[b][:, fc],
                        rhs=ec[:, cols].bitcast(FP8X4),
                        rhs_scale=es[:, cols],
                        start=True,
                        stop=True,
                    )
                live[("ap", i, j)] = ap
            elif kind == "ex":
                if ("xg", i) not in live:
                    live[("xg", i)] = work.tile([P, N, 4], BF16, name="xg", align_bytes=64)
                copy_on(engine, live[("xg", i)][:, j * P:(j + 1) * P, :], live[("ap", i, j)][:].rearrange("p k n -> p n k"))
            elif kind == "qx":
                b = i // 2
                nc.vector.quantize_mx(out=xc[b][:, i % 2, :].bitcast(FP8X4), scales=xs[b][:, i % 2, :], in_=live[("xg", i)][:].rearrange("p n k -> p (n k)"))
            elif kind == "wt":
                wt = psum.tile([P, 2, 2, P], F32, name="wt", tag="ps")
                for s in range(2):
                    w32 = wr[:, 2 * j + s, :].bitcast(F32)
                    for u in range(2):
                        lo = 256 * i + P * u
                        nc.tensor.transpose(wt[:, s, u, :], w32[:, lo:lo + P], ident_f[:])
                live[("wt", i, j)] = wt
            elif kind == "we":
                dst = wg32[:, i, 256 * j:256 * (j + 1), :].rearrange("p (s o) u -> p s o u", s=2)
                copy_on(engine, dst, live[("wt", i, j)][:].rearrange("p s u o -> p s o u"))
            elif kind == "qw":
                nc.vector.quantize_mx(out=wc[:, i, :].bitcast(FP8X4), scales=ws[:, i, :], in_=wg[:, i * 4 * C:(i + 1) * 4 * C])
            elif kind == "z":
                live[("z", i, j)] = z_bank(j, i)
            elif kind == "bn":
                nc.vector.bn_stats(out=st[:, j, i, :], in_=live[("z", i, j)][:])
            elif kind == "ag":
                lo, hi = GROUPS[i], GROUPS[i + 1]
                for O in range(lo, hi):
                    nc.vector.bn_aggr(out=mv[:, O, :], in_=st[:, O, :, :].rearrange("p b s -> p (b s)"))
                nc.vector.scalar_tensor_tensor(out=gm[:, 1, lo:hi], in0=mv[:, lo:hi, 0], scalar=-1.0, in1=gm[:, 0, lo:hi], op0=ALU.mult, op1=ALU.mult)
            elif kind == "sq":
                lo, hi = GROUPS[i], GROUPS[i + 1]
                nc.scalar.activation(out=sd[:, lo:hi], in_=mv[:, lo:hi, 1], func=ACT.Sqrt, bias=eps_t[:, 0:1], scale=1.0)
            elif kind == "c1":
                lo, hi = GROUPS[i], GROUPS[i + 1]
                nc.vector.reciprocal(out=rstd[:, lo:hi], in_=sd[:, lo:hi])
            elif kind == "c2":
                lo, hi = GROUPS[i], GROUPS[i + 1]
                nc.vector.tensor_tensor(out=cc[:, :, lo:hi], in0=gm[:, :, lo:hi], in1=rstd[:, lo:hi].unsqueeze(1).to_broadcast([P, 2, hi - lo]), op=ALU.mult)
            elif kind == "c3":
                lo, hi = GROUPS[i], GROUPS[i + 1]
                if hi - lo == 1:
                    nc.vector.scalar_tensor_tensor(out=cb[:, lo:hi], in0=gm[:, 1, lo:hi], scalar=rstd[:, lo:hi], in1=bT[:, lo:hi], op0=ALU.mult, op1=ALU.add)
                else:
                    nc.vector.tensor_tensor(out=cb[:, lo:hi], in0=bT[:, lo:hi], in1=cc[:, 1, lo:hi], op=ALU.add)
            elif kind == "f":
                live[("f", i, j)] = z_bank(i, j)
            elif kind == "af":
                if ("y", i) not in live:
                    live[("y", i)] = ypool.tile([P, B, N], F32, name="y")
                nc.scalar.activation(out=live[("y", i)][:, j, :], in_=live[("f", i, j)][:], func=ACT.Identity, bias=cb[:, i:i + 1], scale=cc[:, 0, i:i + 1])
            elif kind == "lr":
                y = live[("y", i)]
                if ("yo", i) not in live:
                    live[("yo", i)] = ypool.tile([P, B, N], F32, name="yo")
                yo = live[("yo", i)]
                width = B // PIECES.get(i, 1)
                bs = slice(j * width, (j + 1) * width)
                yf = y[:, bs, :].rearrange("p b n -> p (b n)")
                nc.vector.scalar_tensor_tensor(out=yo[:, bs, :].rearrange("p b n -> p (b n)"), in0=yf, scalar=NEG_SLOPE, in1=yf, op0=ALU.mult, op1=ALU.max)
                nc.sync.dma_start(out=out_view[i][:, bs, :], in_=yo[:, bs, :])

        for kind, i, j, engine in merged(queues()):
            step(kind, i, j, engine)
